import numpy as np
import ml_dtypes


def mxq(x, axis, fmt="e4m3"):
    dtype, down = {"e4m3": (ml_dtypes.float8_e4m3fn, 7), "e5m2": (ml_dtypes.float8_e5m2, 14)}[fmt]
    v = np.moveaxis(np.asarray(x, np.float32).astype(ml_dtypes.bfloat16).astype(np.float64), axis, -1)
    blocks = v.reshape(v.shape[:-1] + (-1, 32))
    amax = np.abs(blocks).max(-1, keepdims=True)
    byte = np.maximum(np.where(amax > 0, np.frexp(amax)[1] - 1 + 127, 0) - down, 1)
    scale = np.exp2(byte - 127.0)
    codes = (blocks / scale).astype(np.float32).astype(dtype).astype(np.float64)
    return np.moveaxis((codes * scale).reshape(v.shape), -1, axis)


WIDE = False


def mx_kscale(k):
    if not WIDE:
        return np.ones(k)
    levels = np.array([10, -10, 5, -5, 0])
    a = np.random.permutation(np.resize(levels, k // 512 * 4)).reshape(k // 512, 4)
    idx = np.arange(k)
    return np.exp2(a[idx // 512, idx % 128 // 32])


BF16 = ml_dtypes.bfloat16


def bf(x):
    return np.asarray(x, np.float32).astype(BF16)


def f64(x):
    return np.asarray(x).astype(np.float64)


B, O, D, G1, G2, F1, F2 = 256, 8, 256, 512, 128, 512, 512
C = D + D
P = O * O


def setup_inputs():
    s = mx_kscale(C)[:D]
    ss = np.concatenate([s, s])
    t = mx_kscale(G1)
    return {
        "objs": bf(np.random.standard_normal((B, O, D)) * s),
        "W1": bf(np.random.standard_normal((G1, C)) / np.sqrt(C) / ss * t[:, None]),
        "b1": bf(np.random.standard_normal(G1) * 0.3 * t),
        "W2": bf(np.random.standard_normal((G2, G1)) * 0.5 / np.sqrt(G1) / t),
        "b2": bf(np.random.standard_normal(G2) * 0.15),
    }


def reference(objs, W1, b1, W2, b2):
    v = f64(objs)
    v_i = np.broadcast_to(v[:, None, :, :], (B, O, O, D))
    v_j = np.broadcast_to(v[:, :, None, :], (B, O, O, D))
    pairs = np.concatenate([v_i, v_j], axis=-1).reshape(B, P, C)
    h = np.maximum((mxq(pairs, 2, "e4m3") @ mxq(f64(W1).T, 0, "e4m3")) + f64(b1), 0.0)
    x_pairs = np.maximum((mxq(h, 2, "e4m3") @ mxq(f64(W2).T, 0, "e4m3")) + f64(b2), 0.0)
    return x_pairs, x_pairs.sum(axis=1)

@@ -1,0 +1,270 @@
+from contextlib import ExitStack
+
+import concourse.mybir as mybir
+from concourse.masks import make_identity
+
+F32 = mybir.dt.float32
+BF16 = mybir.dt.bfloat16
+U32 = mybir.dt.uint32
+I32 = mybir.dt.int32
+U8 = mybir.dt.uint8
+FP8X4 = mybir.dt.float8_e4m3fn_x4
+ACT = mybir.ActivationFunctionType
+ALU = mybir.AluOpType
+
+P = 128
+SETS = 256
+OBJ = 8
+FLOPS = 2 * SETS * OBJ * OBJ * 512 * (512 + 128)
+RELU_ON_VECTOR_EVERY = 2
+
+
+def tile_pairwiserelationmodule_pa_t_kernel(tc, objs, W1, b1, W2, b2, out_0, out_1):
+    nc = tc.nc
+    with ExitStack() as ctx:
+        keep = ctx.enter_context(tc.tile_pool(name="keep", bufs=1))
+        work = ctx.enter_context(tc.tile_pool(name="work", bufs=3))
+        outp = ctx.enter_context(tc.tile_pool(name="outp", bufs=4))
+        ps_x = ctx.enter_context(tc.psum_pool(name="ps_x", bufs=4))
+        ps_y = ctx.enter_context(tc.psum_pool(name="ps_y", bufs=2))
+        ps_s = ctx.enter_context(tc.psum_pool(name="ps_s", bufs=1))
+
+        w1_raw = keep.tile([P, 4 * 768], BF16)
+        w1_raw_v = w1_raw[:].rearrange("p (t k) -> p t k", k=768)
+        w1_rows = W1.rearrange("(p t) k -> p t k", t=4)
+        nc.sync.dma_start(out=w1_raw_v[:, :, 0:512], in_=w1_rows)
+        nc.sync.dma_start(out=w1_raw_v[:, :, 512:768], in_=w1_rows[:, :, 0:256])
+        obj_rows = objs.rearrange("(h p) o d -> h p (o d)", p=P)
+        obj_raw0 = keep.tile([P, 9 * 256], BF16)
+        obj_raw1 = keep.tile([P, 9 * 256], BF16)
+        obj_raw = [obj_raw0, obj_raw1]
+        for h in range(2):
+            nc.sync.dma_start(out=obj_raw[h][:, 0:2048], in_=obj_rows[h])
+        for h in range(2):
+            nc.sync.dma_start(out=obj_raw[h][:, 2048:2304], in_=obj_rows[h][:, 0:256])
+        w2_raw = keep.tile([P, 512], BF16)
+        nc.sync.dma_start(out=w2_raw[:], in_=W2)
+        b1_raw = keep.tile([P, 4], BF16)
+        nc.scalar.dma_start(out=b1_raw[:], in_=b1.rearrange("(p t) -> p t", t=4))
+        b2_raw = keep.tile([P, P], BF16)
+        nc.scalar.dma_start(out=b2_raw[:], in_=b2.partition_broadcast(P))
+
+        ident = keep.tile([P, P], F32)
+        make_identity(nc, ident[:])
+
+        rot_codes = {}
+        rot_scales = {}
+        codes1 = keep.tile([P, OBJ * SETS], U32, align_bytes=64)
+        scales1 = keep.tile([P, OBJ * SETS], U8, align_bytes=64)
+        rot_codes[1] = codes1
+        rot_scales[1] = scales1
+        nc.vector.memset(scales1[:].bitcast(I32), 0)
+
+        w1_grp = keep.tile([P, 2 * 4 * P * 4], BF16, align_bytes=64)
+        w1_grp_v = w1_grp[:].bitcast(F32).rearrange("p (v t c u) -> p v t c u", v=2, t=4, u=2)
+        w1_words = w1_raw[:].bitcast(F32).rearrange("p (t c u) -> p t c u", t=4, u=2)
+        n_copy = 0
+        for arr in range(2):
+            for t0 in (0, 2):
+                pw = ps_x.tile([P, 4, P], F32, tag="x")
+                for dt in range(2):
+                    for u in range(2):
+                        nc.tensor.transpose(
+                            pw[:, 2 * dt + u, :],
+                            w1_words[:, t0 + dt, 64 * arr : 64 * arr + P, u],
+                            ident[:],
+                        )
+                src = pw[:].rearrange("p (t u) c -> p t c u", u=2)
+                dst = w1_grp_v[:, arr, t0 : t0 + 2]
+                if n_copy % 2 == 0:
+                    nc.vector.tensor_copy(out=dst, in_=src)
+                else:
+                    nc.scalar.copy(out=dst, in_=src)
+                n_copy += 1
+        w1_codes = keep.tile([P, 8 * P], U32, align_bytes=64)
+        w1_scales = keep.tile([P, 8 * P], U8, align_bytes=64)
+        nc.vector.quantize_mx(out=w1_codes[:].bitcast(FP8X4), scales=w1_scales[:], in_=w1_grp[:])
+
+        obj_grp = keep.tile([P, OBJ * SETS * 4], BF16, align_bytes=64)
+        obj_grp_v = obj_grp[:].bitcast(F32).rearrange("p (j h c u) -> p j h c u", j=OBJ, h=2, u=2)
+        obj_words = [obj_raw[h][:].bitcast(F32).rearrange("p (c u) -> p c u", u=2) for h in range(2)]
+        for j in range(OBJ):
+            po = ps_x.tile([P, 4, P], F32, tag="x")
+            for h in range(2):
+                for u in range(2):
+                    nc.tensor.transpose(po[:, 2 * h + u, :], obj_words[h][:, 64 * j : 64 * j + P, u], ident[:])
+            src = po[:].rearrange("p (h u) c -> p h c u", u=2)
+            if j % 2 == 0:
+                nc.vector.tensor_copy(out=obj_grp_v[:, j], in_=src)
+            else:
+                nc.scalar.copy(out=obj_grp_v[:, j], in_=src)
+            if j % 2 == 1:
+                c0 = SETS * (j - 1)
+                nc.vector.quantize_mx(
+                    out=codes1[:, c0 : c0 + 512].bitcast(FP8X4),
+                    scales=scales1[:, c0 : c0 + 512],
+                    in_=obj_grp[:, 4 * c0 : 4 * c0 + 2048],
+                )
+
+        w2_grp = keep.tile([P, P * 4], BF16, align_bytes=64)
+        w2_words = w2_raw[:].bitcast(F32).rearrange("p (c u) -> p c u", u=2)
+        p2 = ps_y.tile([P, 4, P], F32, tag="y")
+        for u in range(2):
+            nc.tensor.transpose(p2[:, u, :], w2_words[:, :, u], ident[:])
+        nc.scalar.copy(
+            out=w2_grp[:].bitcast(F32).rearrange("p (c u) -> p c u", u=2),
+            in_=p2[:, 0:2, :].rearrange("p u c -> p c u"),
+        )
+        w2_codes = keep.tile([P, P], U32, align_bytes=64)
+        w2_scales = keep.tile([P, P], U8, align_bytes=64)
+        nc.vector.quantize_mx(out=w2_codes[:].bitcast(FP8X4), scales=w2_scales[:], in_=w2_grp[:])
+
+        b1_f = keep.tile([P, 4], F32)
+        nc.vector.tensor_copy(out=b1_f[:], in_=b1_raw[:])
+        b2_f = keep.tile([P, P], F32)
+        nc.vector.tensor_copy(out=b2_f[:], in_=b2_raw[:])
+
+        for r in (2, 3, 4, 0):
+            rc = keep.tile([P, OBJ * SETS], U32, name="rc%d" % r, align_bytes=64)
+            rs = keep.tile([P, OBJ * SETS], U8, name="rs%d" % r, align_bytes=64)
+            rot_codes[r] = rc
+            rot_scales[r] = rs
+            shift = (r - 1) % OBJ
+            for dst_t, src_t, w in ((rc, codes1, SETS), (rs, scales1, SETS // 4)):
+                dv = dst_t[:].bitcast(I32)
+                sv = src_t[:].bitcast(I32)
+                nc.sync.dma_start(out=dv[0:64, :], in_=sv[0:64, :])
+                cut = (OBJ - shift) * w
+                nc.sync.dma_start(out=dv[64:128, 0:cut], in_=sv[64:128, shift * w : OBJ * w])
+                nc.sync.dma_start(out=dv[64:128, cut : OBJ * w], in_=sv[64:128, 0 : shift * w])
+
+        out_rows = out_0.rearrange("(h p) q g -> p h q g", p=P)
+        sum_t0 = ps_s.tile([P, P], F32)
+        sum_t1 = ps_s.tile([P, P], F32)
+        sum_t = [sum_t0, sum_t1]
+
+        chunks = []
+        for r, swaps in ((1, (0, 1)), (2, (0, 1)), (3, (0, 1)), (4, (0,)), (0, (0,))):
+            for swap in swaps:
+                for jj in range(4):
+                    chunks.append((r, swap, jj))
+        n = len(chunks)
+        st = {}
+
+        def layer1(i):
+            r, swap, jj = chunks[i]
+            hid = work.tile([P, 4, 512], BF16, tag="hid")
+            for t in range(4):
+                x = ps_x.tile([P, 512], F32, tag="x")
+                c0 = (4 * swap + t) * P
+                nc.tensor.matmul_mx(
+                    out=x[:],
+                    lhsT=w1_codes[:, c0 : c0 + P].bitcast(FP8X4),
+                    lhsT_scale=w1_scales[:, c0 : c0 + P],
+                    rhs=rot_codes[r][:, 512 * jj : 512 * jj + 512].bitcast(FP8X4),
+                    rhs_scale=rot_scales[r][:, 512 * jj : 512 * jj + 512],
+                    start=True,
+                    stop=True,
+                )
+                nc.scalar.activation(out=hid[:, t, :], in_=x[:], func=ACT.Relu, bias=b1_f[:, t : t + 1], scale=1.0)
+            st[("hid", i)] = hid
+
+        def regroup(i):
+            hid = st[("hid", i)]
+            grp = work.tile([P, 512, 4], BF16, tag="grp", align_bytes=64)
+            nc.vector.tensor_copy(
+                out=grp[:].rearrange("p (c i) t -> p c t i", i=4),
+                in_=hid[:].rearrange("p t (c i) -> p c t i", i=4),
+            )
+            st[("grp", i)] = grp
+
+        def quantise(i):
+            grp = st[("grp", i)]
+            hc = work.tile([P, 512], U32, tag="hc", align_bytes=64)
+            hs = work.tile([P, 512], U8, tag="hs", align_bytes=64)
+            nc.vector.quantize_mx(out=hc[:].bitcast(FP8X4), scales=hs[:], in_=grp[:].rearrange("p w t -> p (w t)"))
+            st[("h", i)] = (hc, hs)
+
+        def layer2(i):
+            hc, hs = st[("h", i)]
+            y = ps_y.tile([P, 4, P], F32, tag="y")
+            for h in range(2):
+                for q in range(2):
+                    c0 = SETS * q + P * h
+                    nc.tensor.matmul_mx(
+                        out=y[:, 2 * h + q, :],
+                        lhsT=hc[:, c0 : c0 + P].bitcast(FP8X4),
+                        lhsT_scale=hs[:, c0 : c0 + P],
+                        rhs=w2_codes[:].bitcast(FP8X4),
+                        rhs_scale=w2_scales[:],
+                        start=True,
+                        stop=True,
+                    )
+            st[("y", i)] = y
+
+        def bias2(i):
+            y = st[("y", i)]
+            z = work.tile([P, 512], F32, tag="z")
+            nc.vector.tensor_tensor(
+                out=z[:].rearrange("p (j g) -> p j g", g=P),
+                in0=y[:],
+                in1=b2_f[:].unsqueeze(1).to_broadcast([P, 4, P]),
+                op=ALU.add,
+            )
+            st[("z", i)] = z
+
+        def finish(i):
+            r, swap, jj = chunks[i]
+            z = st[("z", i)]
+            xo = outp.tile([P, 512], F32, tag="xo")
+            if i % RELU_ON_VECTOR_EVERY == 0:
+                nc.vector.tensor_scalar_max(out=xo[:], in0=z[:], scalar1=0.0)
+            else:
+                nc.scalar.activation(out=xo[:], in_=z[:], func=ACT.Relu)
+            xo_v = xo[:].rearrange("p (h q g) -> p h q g", h=2, q=2)
+            for q in range(2):
+                top = 2 * jj + q
+                bot = (top + r) % OBJ
+                m, k = (top, bot) if swap == 0 else (bot, top)
+                nc.sync.dma_start(out=out_rows[:, :, OBJ * k + m, :], in_=xo_v[:, :, q, :])
+            st[("xo", i)] = xo
+
+        def add_up(i):
+            xo = st[("xo", i)]
+            for h in range(2):
+                for q in range(2):
+                    c0 = (2 * h + q) * P
+                    nc.tensor.matmul(
+                        out=sum_t[h][:],
+                        lhsT=xo[:, c0 : c0 + P],
+                        rhs=ident[:],
+                        start=(i == 0 and q == 0),
+                        stop=(i == n - 1 and q == 1),
+                        is_transpose=True,
+                    )
+
+        for i in range(n + 4):
+            if i < n:
+                layer1(i)
+            if 0 <= i - 2 < n:
+                layer2(i - 2)
+            if 0 <= i - 4 < n:
+                add_up(i - 4)
+            if 0 <= i - 1 < n:
+                regroup(i - 1)
+            if 0 <= i - 3 < n:
+                bias2(i - 3)
+            if 0 <= i - 1 < n:
+                quantise(i - 1)
+            if 0 <= i - 3 < n:
+                finish(i - 3)
+
+        sum_sb = keep.tile([P, 2, P], F32)
+        nc.vector.tensor_copy(out=sum_sb[:, 0, :], in_=sum_t[0][:])
+        nc.scalar.copy(out=sum_sb[:, 1, :], in_=sum_t[1][:])
+        back = ps_y.tile([P, 4, P], F32, tag="y")
+        for h in range(2):
+            nc.tensor.transpose(back[:, h, :], sum_sb[:, h, :], ident[:])
+        total = keep.tile([P, 2, P], F32)
+        nc.vector.tensor_copy(out=total[:], in_=back[:, 0:2, :])
+        nc.sync.dma_start(out=out_1.rearrange("(h p) g -> p h g", p=P), in_=total[:])

@@ -16,7 +16,6 @@ P = 128
 SETS = 256
 OBJ = 8
 FLOPS = 2 * SETS * OBJ * OBJ * 512 * (512 + 128)
-RELU_ON_VECTOR_EVERY = 2
 
 
 def tile_pairwiserelationmodule_pa_t_kernel(tc, objs, W1, b1, W2, b2, out_0, out_1):
@@ -33,17 +32,19 @@ def tile_pairwiserelationmodule_pa_t_kernel(tc, objs, W1, b1, W2, b2, out_0, out
         w1_raw_v = w1_raw[:].rearrange("p (t k) -> p t k", k=768)
         w1_rows = W1.rearrange("(p t) k -> p t k", t=4)
         nc.sync.dma_start(out=w1_raw_v[:, :, 0:512], in_=w1_rows)
-        nc.sync.dma_start(out=w1_raw_v[:, :, 512:768], in_=w1_rows[:, :, 0:256])
         obj_rows = objs.rearrange("(h p) o d -> h p (o d)", p=P)
         obj_raw0 = keep.tile([P, 9 * 256], BF16)
         obj_raw1 = keep.tile([P, 9 * 256], BF16)
         obj_raw = [obj_raw0, obj_raw1]
         for h in range(2):
-            nc.sync.dma_start(out=obj_raw[h][:, 0:2048], in_=obj_rows[h])
+            nc.sync.dma_start(out=obj_raw[h][:, 0:768], in_=obj_rows[h][:, 0:768])
         for h in range(2):
-            nc.sync.dma_start(out=obj_raw[h][:, 2048:2304], in_=obj_rows[h][:, 0:256])
+            nc.sync.dma_start(out=obj_raw[h][:, 768:2048], in_=obj_rows[h][:, 768:2048])
         w2_raw = keep.tile([P, 512], BF16)
         nc.sync.dma_start(out=w2_raw[:], in_=W2)
+        for h in range(2):
+            nc.sync.dma_start(out=obj_raw[h][:, 2048:2304], in_=obj_rows[h][:, 0:256])
+        nc.sync.dma_start(out=w1_raw_v[:, :, 512:768], in_=w1_rows[:, :, 0:256])
         b1_raw = keep.tile([P, 4], BF16)
         nc.scalar.dma_start(out=b1_raw[:], in_=b1.rearrange("(p t) -> p t", t=4))
         b2_raw = keep.tile([P, P], BF16)
@@ -63,8 +64,10 @@ def tile_pairwiserelationmodule_pa_t_kernel(tc, objs, W1, b1, W2, b2, out_0, out
         w1_grp = keep.tile([P, 2 * 4 * P * 4], BF16, align_bytes=64)
         w1_grp_v = w1_grp[:].bitcast(F32).rearrange("p (v t c u) -> p v t c u", v=2, t=4, u=2)
         w1_words = w1_raw[:].bitcast(F32).rearrange("p (t c u) -> p t c u", t=4, u=2)
-        n_copy = 0
-        for arr in range(2):
+        w1_codes = keep.tile([P, 8 * P], U32, align_bytes=64)
+        w1_scales = keep.tile([P, 8 * P], U8, align_bytes=64)
+
+        def prep_w1(arr):
             for t0 in (0, 2):
                 pw = ps_x.tile([P, 4, P], F32, tag="x")
                 for dt in range(2):
@@ -76,55 +79,59 @@ def tile_pairwiserelationmodule_pa_t_kernel(tc, objs, W1, b1, W2, b2, out_0, out
                         )
                 src = pw[:].rearrange("p (t u) c -> p t c u", u=2)
                 dst = w1_grp_v[:, arr, t0 : t0 + 2]
-                if n_copy % 2 == 0:
+                if t0 == 0:
                     nc.vector.tensor_copy(out=dst, in_=src)
                 else:
                     nc.scalar.copy(out=dst, in_=src)
-                n_copy += 1
-        w1_codes = keep.tile([P, 8 * P], U32, align_bytes=64)
-        w1_scales = keep.tile([P, 8 * P], U8, align_bytes=64)
-        nc.vector.quantize_mx(out=w1_codes[:].bitcast(FP8X4), scales=w1_scales[:], in_=w1_grp[:])
+            nc.vector.quantize_mx(
+                out=w1_codes[:, 512 * arr : 512 * arr + 512].bitcast(FP8X4),
+                scales=w1_scales[:, 512 * arr : 512 * arr + 512],
+                in_=w1_grp[:, 2048 * arr : 2048 * arr + 2048],
+            )
 
         obj_grp = keep.tile([P, OBJ * SETS * 4], BF16, align_bytes=64)
         obj_grp_v = obj_grp[:].bitcast(F32).rearrange("p (j h c u) -> p j h c u", j=OBJ, h=2, u=2)
         obj_words = [obj_raw[h][:].bitcast(F32).rearrange("p (c u) -> p c u", u=2) for h in range(2)]
-        for j in range(OBJ):
-            po = ps_x.tile([P, 4, P], F32, tag="x")
-            for h in range(2):
-                for u in range(2):
-                    nc.tensor.transpose(po[:, 2 * h + u, :], obj_words[h][:, 64 * j : 64 * j + P, u], ident[:])
-            src = po[:].rearrange("p (h u) c -> p h c u", u=2)
-            if j % 2 == 0:
-                nc.vector.tensor_copy(out=obj_grp_v[:, j], in_=src)
-            else:
-                nc.scalar.copy(out=obj_grp_v[:, j], in_=src)
-            if j % 2 == 1:
-                c0 = SETS * (j - 1)
-                nc.vector.quantize_mx(
-                    out=codes1[:, c0 : c0 + 512].bitcast(FP8X4),
-                    scales=scales1[:, c0 : c0 + 512],
-                    in_=obj_grp[:, 4 * c0 : 4 * c0 + 2048],
-                )
+
+        def prep_obj(jj):
+            for j in (2 * jj, 2 * jj + 1):
+                po = ps_x.tile([P, 4, P], F32, tag="x")
+                for h in range(2):
+                    for u in range(2):
+                        nc.tensor.transpose(po[:, 2 * h + u, :], obj_words[h][:, 64 * j : 64 * j + P, u], ident[:])
+                src = po[:].rearrange("p (h u) c -> p h c u", u=2)
+                if j % 2 == 0:
+                    nc.vector.tensor_copy(out=obj_grp_v[:, j], in_=src)
+                else:
+                    nc.scalar.copy(out=obj_grp_v[:, j], in_=src)
+            c0 = 512 * jj
+            nc.vector.quantize_mx(
+                out=codes1[:, c0 : c0 + 512].bitcast(FP8X4),
+                scales=scales1[:, c0 : c0 + 512],
+                in_=obj_grp[:, 4 * c0 : 4 * c0 + 2048],
+            )
 
         w2_grp = keep.tile([P, P * 4], BF16, align_bytes=64)
         w2_words = w2_raw[:].bitcast(F32).rearrange("p (c u) -> p c u", u=2)
-        p2 = ps_y.tile([P, 4, P], F32, tag="y")
-        for u in range(2):
-            nc.tensor.transpose(p2[:, u, :], w2_words[:, :, u], ident[:])
-        nc.scalar.copy(
-            out=w2_grp[:].bitcast(F32).rearrange("p (c u) -> p c u", u=2),
-            in_=p2[:, 0:2, :].rearrange("p u c -> p c u"),
-        )
         w2_codes = keep.tile([P, P], U32, align_bytes=64)
         w2_scales = keep.tile([P, P], U8, align_bytes=64)
-        nc.vector.quantize_mx(out=w2_codes[:].bitcast(FP8X4), scales=w2_scales[:], in_=w2_grp[:])
+
+        def prep_w2():
+            p2 = ps_y.tile([P, 4, P], F32, tag="y")
+            for u in range(2):
+                nc.tensor.transpose(p2[:, u, :], w2_words[:, :, u], ident[:])
+            nc.scalar.copy(
+                out=w2_grp[:].bitcast(F32).rearrange("p (c u) -> p c u", u=2),
+                in_=p2[:, 0:2, :].rearrange("p u c -> p c u"),
+            )
+            nc.vector.quantize_mx(out=w2_codes[:].bitcast(FP8X4), scales=w2_scales[:], in_=w2_grp[:])
 
         b1_f = keep.tile([P, 4], F32)
         nc.vector.tensor_copy(out=b1_f[:], in_=b1_raw[:])
         b2_f = keep.tile([P, P], F32)
         nc.vector.tensor_copy(out=b2_f[:], in_=b2_raw[:])
 
-        for r in (2, 3, 4, 0):
+        def make_rotated(r):
             rc = keep.tile([P, OBJ * SETS], U32, name="rc%d" % r, align_bytes=64)
             rs = keep.tile([P, OBJ * SETS], U8, name="rs%d" % r, align_bytes=64)
             rot_codes[r] = rc
@@ -166,7 +173,12 @@ def tile_pairwiserelationmodule_pa_t_kernel(tc, objs, W1, b1, W2, b2, out_0, out
                     start=True,
                     stop=True,
                 )
-                nc.scalar.activation(out=hid[:, t, :], in_=x[:], func=ACT.Relu, bias=b1_f[:, t : t + 1], scale=1.0)
+                if i == n - 1 and t % 2 == 1:
+                    nc.vector.tensor_scalar(
+                        out=hid[:, t, :], in0=x[:], scalar1=b1_f[:, t : t + 1], scalar2=0.0, op0=ALU.add, op1=ALU.max
+                    )
+                else:
+                    nc.scalar.activation(out=hid[:, t, :], in_=x[:], func=ACT.Relu, bias=b1_f[:, t : t + 1], scale=1.0)
             st[("hid", i)] = hid
 
         def regroup(i):
@@ -217,10 +229,7 @@ def tile_pairwiserelationmodule_pa_t_kernel(tc, objs, W1, b1, W2, b2, out_0, out
             r, swap, jj = chunks[i]
             z = st[("z", i)]
             xo = outp.tile([P, 512], F32, tag="xo")
-            if i % RELU_ON_VECTOR_EVERY == 0:
-                nc.vector.tensor_scalar_max(out=xo[:], in0=z[:], scalar1=0.0)
-            else:
-                nc.scalar.activation(out=xo[:], in_=z[:], func=ACT.Relu)
+            nc.gpsimd.tensor_scalar(out=xo[:], in0=z[:], scalar1=0.0, scalar2=0.0, op0=ALU.max, op1=ALU.add)
             xo_v = xo[:].rearrange("p (h q g) -> p h q g", h=2, q=2)
             for q in range(2):
                 top = 2 * jj + q
@@ -243,7 +252,16 @@ def tile_pairwiserelationmodule_pa_t_kernel(tc, objs, W1, b1, W2, b2, out_0, out
                         is_transpose=True,
                     )
 
+        prep_w1(0)
         for i in range(n + 4):
+            if i < 4:
+                prep_obj(i)
+            if i == 1:
+                prep_w2()
+            if i == 4:
+                prep_w1(1)
+                for r in (2, 3, 4, 0):
+                    make_rotated(r)
             if i < n:
                 layer1(i)
             if 0 <= i - 2 < n:

@@ -16,6 +16,7 @@ P = 128
 SETS = 256
 OBJ = 8
 FLOPS = 2 * SETS * OBJ * OBJ * 512 * (512 + 128)
+RELU_ON_VECTOR_EVERY = 2
 
 
 def tile_pairwiserelationmodule_pa_t_kernel(tc, objs, W1, b1, W2, b2, out_0, out_1):
@@ -23,7 +24,8 @@ def tile_pairwiserelationmodule_pa_t_kernel(tc, objs, W1, b1, W2, b2, out_0, out
     with ExitStack() as ctx:
         keep = ctx.enter_context(tc.tile_pool(name="keep", bufs=1))
         work = ctx.enter_context(tc.tile_pool(name="work", bufs=3))
-        outp = ctx.enter_context(tc.tile_pool(name="outp", bufs=4))
+        outp = ctx.enter_context(tc.tile_pool(name="outp", bufs=8))
+        rotp = ctx.enter_context(tc.tile_pool(name="rotp", bufs=2))
         ps_x = ctx.enter_context(tc.psum_pool(name="ps_x", bufs=4))
         ps_y = ctx.enter_context(tc.psum_pool(name="ps_y", bufs=2))
         ps_s = ctx.enter_context(tc.psum_pool(name="ps_s", bufs=1))
@@ -32,19 +34,17 @@ def tile_pairwiserelationmodule_pa_t_kernel(tc, objs, W1, b1, W2, b2, out_0, out
         w1_raw_v = w1_raw[:].rearrange("p (t k) -> p t k", k=768)
         w1_rows = W1.rearrange("(p t) k -> p t k", t=4)
         nc.sync.dma_start(out=w1_raw_v[:, :, 0:512], in_=w1_rows)
+        nc.sync.dma_start(out=w1_raw_v[:, :, 512:768], in_=w1_rows[:, :, 0:256])
         obj_rows = objs.rearrange("(h p) o d -> h p (o d)", p=P)
         obj_raw0 = keep.tile([P, 9 * 256], BF16)
         obj_raw1 = keep.tile([P, 9 * 256], BF16)
         obj_raw = [obj_raw0, obj_raw1]
         for h in range(2):
-            nc.sync.dma_start(out=obj_raw[h][:, 0:768], in_=obj_rows[h][:, 0:768])
-        for h in range(2):
-            nc.sync.dma_start(out=obj_raw[h][:, 768:2048], in_=obj_rows[h][:, 768:2048])
-        w2_raw = keep.tile([P, 512], BF16)
-        nc.sync.dma_start(out=w2_raw[:], in_=W2)
+            nc.sync.dma_start(out=obj_raw[h][:, 0:2048], in_=obj_rows[h])
         for h in range(2):
             nc.sync.dma_start(out=obj_raw[h][:, 2048:2304], in_=obj_rows[h][:, 0:256])
-        nc.sync.dma_start(out=w1_raw_v[:, :, 512:768], in_=w1_rows[:, :, 0:256])
+        w2_raw = keep.tile([P, 512], BF16)
+        nc.sync.dma_start(out=w2_raw[:], in_=W2)
         b1_raw = keep.tile([P, 4], BF16)
         nc.scalar.dma_start(out=b1_raw[:], in_=b1.rearrange("(p t) -> p t", t=4))
         b2_raw = keep.tile([P, P], BF16)
@@ -64,10 +64,8 @@ def tile_pairwiserelationmodule_pa_t_kernel(tc, objs, W1, b1, W2, b2, out_0, out
         w1_grp = keep.tile([P, 2 * 4 * P * 4], BF16, align_bytes=64)
         w1_grp_v = w1_grp[:].bitcast(F32).rearrange("p (v t c u) -> p v t c u", v=2, t=4, u=2)
         w1_words = w1_raw[:].bitcast(F32).rearrange("p (t c u) -> p t c u", t=4, u=2)
-        w1_codes = keep.tile([P, 8 * P], U32, align_bytes=64)
-        w1_scales = keep.tile([P, 8 * P], U8, align_bytes=64)
-
-        def prep_w1(arr):
+        n_copy = 0
+        for arr in range(2):
             for t0 in (0, 2):
                 pw = ps_x.tile([P, 4, P], F32, tag="x")
                 for dt in range(2):
@@ -79,61 +77,57 @@ def tile_pairwiserelationmodule_pa_t_kernel(tc, objs, W1, b1, W2, b2, out_0, out
                         )
                 src = pw[:].rearrange("p (t u) c -> p t c u", u=2)
                 dst = w1_grp_v[:, arr, t0 : t0 + 2]
-                if t0 == 0:
+                if n_copy % 2 == 0:
                     nc.vector.tensor_copy(out=dst, in_=src)
                 else:
                     nc.scalar.copy(out=dst, in_=src)
-            nc.vector.quantize_mx(
-                out=w1_codes[:, 512 * arr : 512 * arr + 512].bitcast(FP8X4),
-                scales=w1_scales[:, 512 * arr : 512 * arr + 512],
-                in_=w1_grp[:, 2048 * arr : 2048 * arr + 2048],
-            )
+                n_copy += 1
+        w1_codes = keep.tile([P, 8 * P], U32, align_bytes=64)
+        w1_scales = keep.tile([P, 8 * P], U8, align_bytes=64)
+        nc.vector.quantize_mx(out=w1_codes[:].bitcast(FP8X4), scales=w1_scales[:], in_=w1_grp[:])
 
         obj_grp = keep.tile([P, OBJ * SETS * 4], BF16, align_bytes=64)
         obj_grp_v = obj_grp[:].bitcast(F32).rearrange("p (j h c u) -> p j h c u", j=OBJ, h=2, u=2)
         obj_words = [obj_raw[h][:].bitcast(F32).rearrange("p (c u) -> p c u", u=2) for h in range(2)]
-
-        def prep_obj(jj):
-            for j in (2 * jj, 2 * jj + 1):
-                po = ps_x.tile([P, 4, P], F32, tag="x")
-                for h in range(2):
-                    for u in range(2):
-                        nc.tensor.transpose(po[:, 2 * h + u, :], obj_words[h][:, 64 * j : 64 * j + P, u], ident[:])
-                src = po[:].rearrange("p (h u) c -> p h c u", u=2)
-                if j % 2 == 0:
-                    nc.vector.tensor_copy(out=obj_grp_v[:, j], in_=src)
-                else:
-                    nc.scalar.copy(out=obj_grp_v[:, j], in_=src)
-            c0 = 512 * jj
-            nc.vector.quantize_mx(
-                out=codes1[:, c0 : c0 + 512].bitcast(FP8X4),
-                scales=scales1[:, c0 : c0 + 512],
-                in_=obj_grp[:, 4 * c0 : 4 * c0 + 2048],
-            )
+        for j in range(OBJ):
+            po = ps_x.tile([P, 4, P], F32, tag="x")
+            for h in range(2):
+                for u in range(2):
+                    nc.tensor.transpose(po[:, 2 * h + u, :], obj_words[h][:, 64 * j : 64 * j + P, u], ident[:])
+            src = po[:].rearrange("p (h u) c -> p h c u", u=2)
+            if j % 2 == 0:
+                nc.vector.tensor_copy(out=obj_grp_v[:, j], in_=src)
+            else:
+                nc.scalar.copy(out=obj_grp_v[:, j], in_=src)
+            if j % 2 == 1:
+                c0 = SETS * (j - 1)
+                nc.vector.quantize_mx(
+                    out=codes1[:, c0 : c0 + 512].bitcast(FP8X4),
+                    scales=scales1[:, c0 : c0 + 512],
+                    in_=obj_grp[:, 4 * c0 : 4 * c0 + 2048],
+                )
 
         w2_grp = keep.tile([P, P * 4], BF16, align_bytes=64)
         w2_words = w2_raw[:].bitcast(F32).rearrange("p (c u) -> p c u", u=2)
+        p2 = ps_y.tile([P, 4, P], F32, tag="y")
+        for u in range(2):
+            nc.tensor.transpose(p2[:, u, :], w2_words[:, :, u], ident[:])
+        nc.scalar.copy(
+            out=w2_grp[:].bitcast(F32).rearrange("p (c u) -> p c u", u=2),
+            in_=p2[:, 0:2, :].rearrange("p u c -> p c u"),
+        )
         w2_codes = keep.tile([P, P], U32, align_bytes=64)
         w2_scales = keep.tile([P, P], U8, align_bytes=64)
-
-        def prep_w2():
-            p2 = ps_y.tile([P, 4, P], F32, tag="y")
-            for u in range(2):
-                nc.tensor.transpose(p2[:, u, :], w2_words[:, :, u], ident[:])
-            nc.scalar.copy(
-                out=w2_grp[:].bitcast(F32).rearrange("p (c u) -> p c u", u=2),
-                in_=p2[:, 0:2, :].rearrange("p u c -> p c u"),
-            )
-            nc.vector.quantize_mx(out=w2_codes[:].bitcast(FP8X4), scales=w2_scales[:], in_=w2_grp[:])
+        nc.vector.quantize_mx(out=w2_codes[:].bitcast(FP8X4), scales=w2_scales[:], in_=w2_grp[:])
 
         b1_f = keep.tile([P, 4], F32)
         nc.vector.tensor_copy(out=b1_f[:], in_=b1_raw[:])
         b2_f = keep.tile([P, P], F32)
         nc.vector.tensor_copy(out=b2_f[:], in_=b2_raw[:])
 
-        def make_rotated(r):
-            rc = keep.tile([P, OBJ * SETS], U32, name="rc%d" % r, align_bytes=64)
-            rs = keep.tile([P, OBJ * SETS], U8, name="rs%d" % r, align_bytes=64)
+        for r in (2, 3, 4, 0):
+            rc = rotp.tile([P, OBJ * SETS], U32, tag="rc", align_bytes=64)
+            rs = rotp.tile([P, OBJ * SETS], U8, tag="rs", align_bytes=64)
             rot_codes[r] = rc
             rot_scales[r] = rs
             shift = (r - 1) % OBJ
@@ -173,12 +167,7 @@ def tile_pairwiserelationmodule_pa_t_kernel(tc, objs, W1, b1, W2, b2, out_0, out
                     start=True,
                     stop=True,
                 )
-                if i == n - 1 and t % 2 == 1:
-                    nc.vector.tensor_scalar(
-                        out=hid[:, t, :], in0=x[:], scalar1=b1_f[:, t : t + 1], scalar2=0.0, op0=ALU.add, op1=ALU.max
-                    )
-                else:
-                    nc.scalar.activation(out=hid[:, t, :], in_=x[:], func=ACT.Relu, bias=b1_f[:, t : t + 1], scale=1.0)
+                nc.scalar.activation(out=hid[:, t, :], in_=x[:], func=ACT.Relu, bias=b1_f[:, t : t + 1], scale=1.0)
             st[("hid", i)] = hid
 
         def regroup(i):
@@ -229,7 +218,10 @@ def tile_pairwiserelationmodule_pa_t_kernel(tc, objs, W1, b1, W2, b2, out_0, out
             r, swap, jj = chunks[i]
             z = st[("z", i)]
             xo = outp.tile([P, 512], F32, tag="xo")
-            nc.gpsimd.tensor_scalar(out=xo[:], in0=z[:], scalar1=0.0, scalar2=0.0, op0=ALU.max, op1=ALU.add)
+            if i % RELU_ON_VECTOR_EVERY == 0:
+                nc.vector.tensor_scalar_max(out=xo[:], in0=z[:], scalar1=0.0)
+            else:
+                nc.scalar.activation(out=xo[:], in_=z[:], func=ACT.Relu)
             xo_v = xo[:].rearrange("p (h q g) -> p h q g", h=2, q=2)
             for q in range(2):
                 top = 2 * jj + q
@@ -252,16 +244,7 @@ def tile_pairwiserelationmodule_pa_t_kernel(tc, objs, W1, b1, W2, b2, out_0, out
                         is_transpose=True,
                     )
 
-        prep_w1(0)
         for i in range(n + 4):
-            if i < 4:
-                prep_obj(i)
-            if i == 1:
-                prep_w2()
-            if i == 4:
-                prep_w1(1)
-                for r in (2, 3, 4, 0):
-                    make_rotated(r)
             if i < n:
                 layer1(i)
             if 0 <= i - 2 < n:

@@ -23,26 +23,22 @@ def tile_pairwiserelationmodule_pa_t_kernel(tc, objs, W1, b1, W2, b2, out_0, out
     nc = tc.nc
     with ExitStack() as ctx:
         keep = ctx.enter_context(tc.tile_pool(name="keep", bufs=1))
-        work = ctx.enter_context(tc.tile_pool(name="work", bufs=3))
+        work = ctx.enter_context(tc.tile_pool(name="work", bufs=4))
         outp = ctx.enter_context(tc.tile_pool(name="outp", bufs=8))
-        rotp = ctx.enter_context(tc.tile_pool(name="rotp", bufs=2))
+        rotp = ctx.enter_context(tc.tile_pool(name="rotp", bufs=3))
         ps_x = ctx.enter_context(tc.psum_pool(name="ps_x", bufs=4))
         ps_y = ctx.enter_context(tc.psum_pool(name="ps_y", bufs=2))
         ps_s = ctx.enter_context(tc.psum_pool(name="ps_s", bufs=1))
+        ctx.enter_context(tc.manual_schedule())
 
-        w1_raw = keep.tile([P, 4 * 768], BF16)
-        w1_raw_v = w1_raw[:].rearrange("p (t k) -> p t k", k=768)
-        w1_rows = W1.rearrange("(p t) k -> p t k", t=4)
-        nc.sync.dma_start(out=w1_raw_v[:, :, 0:512], in_=w1_rows)
-        nc.sync.dma_start(out=w1_raw_v[:, :, 512:768], in_=w1_rows[:, :, 0:256])
+        w1_raw = keep.tile([P, 4 * 512], BF16)
+        nc.sync.dma_start(out=w1_raw[:], in_=W1.rearrange("(p t) k -> p (t k)", t=4))
         obj_rows = objs.rearrange("(h p) o d -> h p (o d)", p=P)
-        obj_raw0 = keep.tile([P, 9 * 256], BF16)
-        obj_raw1 = keep.tile([P, 9 * 256], BF16)
+        obj_raw0 = keep.tile([P, 2048], BF16)
+        obj_raw1 = keep.tile([P, 2048], BF16)
         obj_raw = [obj_raw0, obj_raw1]
         for h in range(2):
-            nc.sync.dma_start(out=obj_raw[h][:, 0:2048], in_=obj_rows[h])
-        for h in range(2):
-            nc.sync.dma_start(out=obj_raw[h][:, 2048:2304], in_=obj_rows[h][:, 0:256])
+            nc.sync.dma_start(out=obj_raw[h][:], in_=obj_rows[h])
         w2_raw = keep.tile([P, 512], BF16)
         nc.sync.dma_start(out=w2_raw[:], in_=W2)
         b1_raw = keep.tile([P, 4], BF16)
@@ -60,72 +56,87 @@ def tile_pairwiserelationmodule_pa_t_kernel(tc, objs, W1, b1, W2, b2, out_0, out
         rot_codes[1] = codes1
         rot_scales[1] = scales1
         nc.vector.memset(scales1[:].bitcast(I32), 0)
+        w1_codes0 = keep.tile([P, 4 * P], U32, align_bytes=64)
+        w1_scales0 = keep.tile([P, 4 * P], U8, align_bytes=64)
+        w1_codes1 = keep.tile([P, 4 * P], U32, align_bytes=64)
+        w1_scales1 = keep.tile([P, 4 * P], U8, align_bytes=64)
+        w1_codes = [w1_codes0, w1_codes1]
+        w1_scales = [w1_scales0, w1_scales1]
+        nc.vector.memset(w1_scales0[:].bitcast(I32), 0)
 
-        w1_grp = keep.tile([P, 2 * 4 * P * 4], BF16, align_bytes=64)
-        w1_grp_v = w1_grp[:].bitcast(F32).rearrange("p (v t c u) -> p v t c u", v=2, t=4, u=2)
+        w1_grp = keep.tile([P, 4 * P * 4], BF16, align_bytes=64)
+        w1_grp_v = w1_grp[:].bitcast(F32).rearrange("p (t c u) -> p t c u", t=4, u=2)
         w1_words = w1_raw[:].bitcast(F32).rearrange("p (t c u) -> p t c u", t=4, u=2)
-        n_copy = 0
-        for arr in range(2):
-            for t0 in (0, 2):
-                pw = ps_x.tile([P, 4, P], F32, tag="x")
-                for dt in range(2):
-                    for u in range(2):
-                        nc.tensor.transpose(
-                            pw[:, 2 * dt + u, :],
-                            w1_words[:, t0 + dt, 64 * arr : 64 * arr + P, u],
-                            ident[:],
-                        )
-                src = pw[:].rearrange("p (t u) c -> p t c u", u=2)
-                dst = w1_grp_v[:, arr, t0 : t0 + 2]
-                if n_copy % 2 == 0:
-                    nc.vector.tensor_copy(out=dst, in_=src)
-                else:
-                    nc.scalar.copy(out=dst, in_=src)
-                n_copy += 1
-        w1_codes = keep.tile([P, 8 * P], U32, align_bytes=64)
-        w1_scales = keep.tile([P, 8 * P], U8, align_bytes=64)
-        nc.vector.quantize_mx(out=w1_codes[:].bitcast(FP8X4), scales=w1_scales[:], in_=w1_grp[:])
-
-        obj_grp = keep.tile([P, OBJ * SETS * 4], BF16, align_bytes=64)
-        obj_grp_v = obj_grp[:].bitcast(F32).rearrange("p (j h c u) -> p j h c u", j=OBJ, h=2, u=2)
-        obj_words = [obj_raw[h][:].bitcast(F32).rearrange("p (c u) -> p c u", u=2) for h in range(2)]
-        for j in range(OBJ):
-            po = ps_x.tile([P, 4, P], F32, tag="x")
-            for h in range(2):
-                for u in range(2):
-                    nc.tensor.transpose(po[:, 2 * h + u, :], obj_words[h][:, 64 * j : 64 * j + P, u], ident[:])
-            src = po[:].rearrange("p (h u) c -> p h c u", u=2)
-            if j % 2 == 0:
-                nc.vector.tensor_copy(out=obj_grp_v[:, j], in_=src)
-            else:
-                nc.scalar.copy(out=obj_grp_v[:, j], in_=src)
-            if j % 2 == 1:
-                c0 = SETS * (j - 1)
-                nc.vector.quantize_mx(
-                    out=codes1[:, c0 : c0 + 512].bitcast(FP8X4),
-                    scales=scales1[:, c0 : c0 + 512],
-                    in_=obj_grp[:, 4 * c0 : 4 * c0 + 2048],
-                )
-
+        obj_grp = keep.tile([P, 4 * SETS * 4], BF16, align_bytes=64)
+        obj_grp_v = obj_grp[:].bitcast(F32).rearrange("p (s h c u) -> p s h c u", s=4, h=2, u=2)
+        obj_words = [obj_raw[h][:].bitcast(F32).rearrange("p (s c u) -> p s c u", s=4, u=2) for h in range(2)]
         w2_grp = keep.tile([P, P * 4], BF16, align_bytes=64)
         w2_words = w2_raw[:].bitcast(F32).rearrange("p (c u) -> p c u", u=2)
-        p2 = ps_y.tile([P, 4, P], F32, tag="y")
-        for u in range(2):
-            nc.tensor.transpose(p2[:, u, :], w2_words[:, :, u], ident[:])
-        nc.scalar.copy(
-            out=w2_grp[:].bitcast(F32).rearrange("p (c u) -> p c u", u=2),
-            in_=p2[:, 0:2, :].rearrange("p u c -> p c u"),
-        )
         w2_codes = keep.tile([P, P], U32, align_bytes=64)
         w2_scales = keep.tile([P, P], U8, align_bytes=64)
-        nc.vector.quantize_mx(out=w2_codes[:].bitcast(FP8X4), scales=w2_scales[:], in_=w2_grp[:])
-
         b1_f = keep.tile([P, 4], F32)
-        nc.vector.tensor_copy(out=b1_f[:], in_=b1_raw[:])
         b2_f = keep.tile([P, P], F32)
+
+        def copy_out(engine, dst, src):
+            if engine == "v":
+                nc.vector.tensor_copy(out=dst, in_=src)
+            else:
+                nc.scalar.copy(out=dst, in_=src)
+
+        def obj_quantise(s):
+            nc.vector.quantize_mx(
+                out=codes1[:, 512 * s : 512 * s + SETS].bitcast(FP8X4),
+                scales=scales1[:, 512 * s : 512 * s + SETS],
+                in_=obj_grp[:, 1024 * s : 1024 * s + 1024],
+            )
+
+        w1_banks = []
+        for t0 in (0, 2):
+            pw = ps_x.tile([P, 4, P], F32, tag="x")
+            for dt in range(2):
+                for u in range(2):
+                    nc.tensor.transpose(pw[:, 2 * dt + u, :], w1_words[:, t0 + dt, :, u], ident[:])
+            w1_banks.append(pw)
+        obj_banks = []
+        for s in range(4):
+            if s < 2:
+                po = ps_x.tile([P, 4, P], F32, tag="x")
+            else:
+                po = ps_y.tile([P, 4, P], F32, tag="y")
+            for h in range(2):
+                for u in range(2):
+                    nc.tensor.transpose(po[:, 2 * h + u, :], obj_words[h][:, s, :, u], ident[:])
+            obj_banks.append(po)
+        for which, engine in ((0, "v"), (1, "s")):
+            copy_out(engine, w1_grp_v[:, 2 * which : 2 * which + 2], w1_banks[which][:].rearrange("p (t u) c -> p t c u", u=2))
+        for s, engine in ((0, "v"), (1, "s")):
+            copy_out(engine, obj_grp_v[:, s], obj_banks[s][:].rearrange("p (h u) c -> p h c u", u=2))
+        nc.vector.quantize_mx(out=w1_codes0[:].bitcast(FP8X4), scales=w1_scales0[:], in_=w1_grp[:])
+        for dst_t, src_t in ((w1_codes1, w1_codes0), (w1_scales1, w1_scales0)):
+            dv = dst_t[:].bitcast(I32)
+            sv = src_t[:].bitcast(I32)
+            nc.sync.dma_start(out=dv[0:64, :], in_=sv[64:128, :])
+            nc.sync.dma_start(out=dv[64:128, :], in_=sv[0:64, :])
+        obj_quantise(0)
+        obj_quantise(1)
+        nc.vector.tensor_copy(out=b1_f[:], in_=b1_raw[:])
+        p2 = ps_x.tile([P, 4, P], F32, tag="x")
+        for u in range(2):
+            nc.tensor.transpose(p2[:, u, :], w2_words[:, :, u], ident[:])
+        for s, engine in ((2, "v"), (3, "s")):
+            copy_out(engine, obj_grp_v[:, s], obj_banks[s][:].rearrange("p (h u) c -> p h c u", u=2))
+        copy_out("s", w2_grp[:].bitcast(F32).rearrange("p (c u) -> p c u", u=2), p2[:, 0:2, :].rearrange("p u c -> p c u"))
+        obj_quantise(2)
+        obj_quantise(3)
+        for t_ in (codes1, scales1):
+            v4 = t_[:].bitcast(I32).rearrange("p (s e w) -> p s e w", s=4, e=2)
+            nc.sync.dma_start(out=v4[0:64, :, 1, :], in_=v4[64:128, :, 0, :])
+            nc.sync.dma_start(out=v4[64:128, 0:3, 1, :], in_=v4[0:64, 1:4, 0, :])
+            nc.sync.dma_start(out=v4[64:128, 3, 1, :], in_=v4[0:64, 0, 0, :])
+        nc.vector.quantize_mx(out=w2_codes[:].bitcast(FP8X4), scales=w2_scales[:], in_=w2_grp[:])
         nc.vector.tensor_copy(out=b2_f[:], in_=b2_raw[:])
 
-        for r in (2, 3, 4, 0):
+        def make_rotated(r):
             rc = rotp.tile([P, OBJ * SETS], U32, tag="rc", align_bytes=64)
             rs = rotp.tile([P, OBJ * SETS], U8, tag="rs", align_bytes=64)
             rot_codes[r] = rc
@@ -145,29 +156,42 @@ def tile_pairwiserelationmodule_pa_t_kernel(tc, objs, W1, b1, W2, b2, out_0, out
         sum_t = [sum_t0, sum_t1]
 
         chunks = []
-        for r, swaps in ((1, (0, 1)), (2, (0, 1)), (3, (0, 1)), (4, (0,)), (0, (0,))):
+        for blocks in (((0, 2), (4, 6)), ((1, 3), (5, 7))):
+            for swap in (0, 1):
+                for pair_of_blocks in blocks:
+                    chunks.append((1, swap, pair_of_blocks))
+        for r, swaps in ((2, (0, 1)), (3, (0, 1)), (4, (0,)), (0, (0,))):
             for swap in swaps:
                 for jj in range(4):
-                    chunks.append((r, swap, jj))
+                    chunks.append((r, swap, (2 * jj, 2 * jj + 1)))
         n = len(chunks)
         st = {}
 
         def layer1(i):
-            r, swap, jj = chunks[i]
+            r, swap, (ja, jb) = chunks[i]
             hid = work.tile([P, 4, 512], BF16, tag="hid")
+            if jb == ja + 1:
+                parts = ((0, 512, SETS * ja),)
+            else:
+                parts = ((0, SETS, SETS * ja), (SETS, SETS, SETS * jb))
             for t in range(4):
                 x = ps_x.tile([P, 512], F32, tag="x")
-                c0 = (4 * swap + t) * P
-                nc.tensor.matmul_mx(
-                    out=x[:],
-                    lhsT=w1_codes[:, c0 : c0 + P].bitcast(FP8X4),
-                    lhsT_scale=w1_scales[:, c0 : c0 + P],
-                    rhs=rot_codes[r][:, 512 * jj : 512 * jj + 512].bitcast(FP8X4),
-                    rhs_scale=rot_scales[r][:, 512 * jj : 512 * jj + 512],
-                    start=True,
-                    stop=True,
-                )
-                nc.scalar.activation(out=hid[:, t, :], in_=x[:], func=ACT.Relu, bias=b1_f[:, t : t + 1], scale=1.0)
+                for o0, width, c0 in parts:
+                    nc.tensor.matmul_mx(
+                        out=x[:, o0 : o0 + width],
+                        lhsT=w1_codes[swap][:, P * t : P * t + P].bitcast(FP8X4),
+                        lhsT_scale=w1_scales[swap][:, P * t : P * t + P],
+                        rhs=rot_codes[r][:, c0 : c0 + width].bitcast(FP8X4),
+                        rhs_scale=rot_scales[r][:, c0 : c0 + width],
+                        start=True,
+                        stop=True,
+                    )
+                if i == n - 1 and t % 2 == 1:
+                    nc.vector.tensor_scalar(
+                        out=hid[:, t, :], in0=x[:], scalar1=b1_f[:, t : t + 1], scalar2=0.0, op0=ALU.add, op1=ALU.max
+                    )
+                else:
+                    nc.scalar.activation(out=hid[:, t, :], in_=x[:], func=ACT.Relu, bias=b1_f[:, t : t + 1], scale=1.0)
             st[("hid", i)] = hid
 
         def regroup(i):
@@ -215,16 +239,16 @@ def tile_pairwiserelationmodule_pa_t_kernel(tc, objs, W1, b1, W2, b2, out_0, out
             st[("z", i)] = z
 
         def finish(i):
-            r, swap, jj = chunks[i]
+            r, swap, blocks = chunks[i]
             z = st[("z", i)]
             xo = outp.tile([P, 512], F32, tag="xo")
-            if i % RELU_ON_VECTOR_EVERY == 0:
+            if i % RELU_ON_VECTOR_EVERY == 0 and i < n - 4:
                 nc.vector.tensor_scalar_max(out=xo[:], in0=z[:], scalar1=0.0)
             else:
                 nc.scalar.activation(out=xo[:], in_=z[:], func=ACT.Relu)
             xo_v = xo[:].rearrange("p (h q g) -> p h q g", h=2, q=2)
             for q in range(2):
-                top = 2 * jj + q
+                top = blocks[q]
                 bot = (top + r) % OBJ
                 m, k = (top, bot) if swap == 0 else (bot, top)
                 nc.sync.dma_start(out=out_rows[:, :, OBJ * k + m, :], in_=xo_v[:, :, q, :])
@@ -244,21 +268,24 @@ def tile_pairwiserelationmodule_pa_t_kernel(tc, objs, W1, b1, W2, b2, out_0, out
                         is_transpose=True,
                     )
 
-        for i in range(n + 4):
+        rotate_at = {0: 2, 6: 3, 12: 4, 17: 0}
+        for i in range(n + 7):
+            if i in rotate_at:
+                make_rotated(rotate_at[i])
             if i < n:
                 layer1(i)
-            if 0 <= i - 2 < n:
-                layer2(i - 2)
-            if 0 <= i - 4 < n:
-                add_up(i - 4)
+            if 0 <= i - 3 < n:
+                layer2(i - 3)
+            if 0 <= i - 6 < n:
+                add_up(i - 6)
             if 0 <= i - 1 < n:
                 regroup(i - 1)
-            if 0 <= i - 3 < n:
-                bias2(i - 3)
+            if 0 <= i - 4 < n:
+                bias2(i - 4)
             if 0 <= i - 1 < n:
                 quantise(i - 1)
-            if 0 <= i - 3 < n:
-                finish(i - 3)
+            if 0 <= i - 5 < n:
+                finish(i - 5)
 
         sum_sb = keep.tile([P, 2, P], F32)
         nc.vector.tensor_copy(out=sum_sb[:, 0, :], in_=sum_t[0][:])

@@ -42,9 +42,9 @@ def tile_pairwiserelationmodule_pa_t_kernel(tc, objs, W1, b1, W2, b2, out_0, out
         w2_raw = keep.tile([P, 512], BF16)
         nc.sync.dma_start(out=w2_raw[:], in_=W2)
         b1_raw = keep.tile([P, 4], BF16)
-        nc.scalar.dma_start(out=b1_raw[:], in_=b1.rearrange("(p t) -> p t", t=4))
+        nc.sync.dma_start(out=b1_raw[:], in_=b1.rearrange("(p t) -> p t", t=4))
         b2_raw = keep.tile([P, P], BF16)
-        nc.scalar.dma_start(out=b2_raw[:], in_=b2.partition_broadcast(P))
+        nc.sync.dma_start(out=b2_raw[:], in_=b2.partition_broadcast(P))
 
         ident = keep.tile([P, P], F32)
         make_identity(nc, ident[:])

@@ -34,11 +34,14 @@ def tile_pairwiserelationmodule_pa_t_kernel(tc, objs, W1, b1, W2, b2, out_0, out
         w1_raw = keep.tile([P, 4 * 512], BF16)
         nc.sync.dma_start(out=w1_raw[:], in_=W1.rearrange("(p t) k -> p (t k)", t=4))
         obj_rows = objs.rearrange("(h p) o d -> h p (o d)", p=P)
-        obj_raw0 = keep.tile([P, 2048], BF16)
-        obj_raw1 = keep.tile([P, 2048], BF16)
-        obj_raw = [obj_raw0, obj_raw1]
-        for h in range(2):
-            nc.sync.dma_start(out=obj_raw[h][:], in_=obj_rows[h])
+        obj_raw00 = keep.tile([P, 1024], BF16)
+        obj_raw01 = keep.tile([P, 1024], BF16)
+        obj_raw10 = keep.tile([P, 1024], BF16)
+        obj_raw11 = keep.tile([P, 1024], BF16)
+        obj_raw = [[obj_raw00, obj_raw01], [obj_raw10, obj_raw11]]
+        for half in range(2):
+            for h in range(2):
+                nc.sync.dma_start(out=obj_raw[half][h][:], in_=obj_rows[h, :, 1024 * half : 1024 * half + 1024])
         w2_raw = keep.tile([P, 512], BF16)
         nc.sync.dma_start(out=w2_raw[:], in_=W2)
         b1_raw = keep.tile([P, 4], BF16)
@@ -69,7 +72,10 @@ def tile_pairwiserelationmodule_pa_t_kernel(tc, objs, W1, b1, W2, b2, out_0, out
         w1_words = w1_raw[:].bitcast(F32).rearrange("p (t c u) -> p t c u", t=4, u=2)
         obj_grp = keep.tile([P, 4 * SETS * 4], BF16, align_bytes=64)
         obj_grp_v = obj_grp[:].bitcast(F32).rearrange("p (s h c u) -> p s h c u", s=4, h=2, u=2)
-        obj_words = [obj_raw[h][:].bitcast(F32).rearrange("p (s c u) -> p s c u", s=4, u=2) for h in range(2)]
+        obj_words = [
+            [obj_raw[half][h][:].bitcast(F32).rearrange("p (s c u) -> p s c u", s=2, u=2) for h in range(2)]
+            for half in range(2)
+        ]
         w2_grp = keep.tile([P, P * 4], BF16, align_bytes=64)
         w2_words = w2_raw[:].bitcast(F32).rearrange("p (c u) -> p c u", u=2)
         w2_codes = keep.tile([P, P], U32, align_bytes=64)
@@ -105,7 +111,7 @@ def tile_pairwiserelationmodule_pa_t_kernel(tc, objs, W1, b1, W2, b2, out_0, out
                 po = ps_y.tile([P, 4, P], F32, tag="y")
             for h in range(2):
                 for u in range(2):
-                    nc.tensor.transpose(po[:, 2 * h + u, :], obj_words[h][:, s, :, u], ident[:])
+                    nc.tensor.transpose(po[:, 2 * h + u, :], obj_words[s // 2][h][:, s % 2, :, u], ident[:])
             obj_banks.append(po)
         for which, engine in ((0, "v"), (1, "s")):
             copy_out(engine, w1_grp_v[:, 2 * which : 2 * which + 2], w1_banks[which][:].rearrange("p (t u) c -> p t c u", u=2))
@@ -120,12 +126,8 @@ def tile_pairwiserelationmodule_pa_t_kernel(tc, objs, W1, b1, W2, b2, out_0, out
         obj_quantise(0)
         obj_quantise(1)
         nc.vector.tensor_copy(out=b1_f[:], in_=b1_raw[:])
-        p2 = ps_x.tile([P, 4, P], F32, tag="x")
-        for u in range(2):
-            nc.tensor.transpose(p2[:, u, :], w2_words[:, :, u], ident[:])
         for s, engine in ((2, "v"), (3, "s")):
             copy_out(engine, obj_grp_v[:, s], obj_banks[s][:].rearrange("p (h u) c -> p h c u", u=2))
-        copy_out("s", w2_grp[:].bitcast(F32).rearrange("p (c u) -> p c u", u=2), p2[:, 0:2, :].rearrange("p u c -> p c u"))
         obj_quantise(2)
         obj_quantise(3)
         for t_ in (codes1, scales1):
@@ -133,9 +135,6 @@ def tile_pairwiserelationmodule_pa_t_kernel(tc, objs, W1, b1, W2, b2, out_0, out
             nc.sync.dma_start(out=v4[0:64, :, 1, :], in_=v4[64:128, :, 0, :])
             nc.sync.dma_start(out=v4[64:128, 0:3, 1, :], in_=v4[0:64, 1:4, 0, :])
             nc.sync.dma_start(out=v4[64:128, 3, 1, :], in_=v4[0:64, 0, 0, :])
-        nc.vector.quantize_mx(out=w2_codes[:].bitcast(FP8X4), scales=w2_scales[:], in_=w2_grp[:])
-        nc.vector.tensor_copy(out=b2_f[:], in_=b2_raw[:])
-
         def make_rotated(r):
             rc = rotp.tile([P, OBJ * SETS], U32, tag="rc", align_bytes=64)
             rs = rotp.tile([P, OBJ * SETS], U8, tag="rs", align_bytes=64)
@@ -164,60 +163,71 @@ def tile_pairwiserelationmodule_pa_t_kernel(tc, objs, W1, b1, W2, b2, out_0, out
             for swap in swaps:
                 for jj in range(4):
                     chunks.append((r, swap, (2 * jj, 2 * jj + 1)))
+        r_last, swap_last, blocks_last = chunks.pop()
+        for block in blocks_last:
+            chunks.append((r_last, swap_last, (block,)))
         n = len(chunks)
         st = {}
 
         def layer1(i):
-            r, swap, (ja, jb) = chunks[i]
+            r, swap, blocks = chunks[i]
+            width = SETS * len(blocks)
             hid = work.tile([P, 4, 512], BF16, tag="hid")
-            if jb == ja + 1:
-                parts = ((0, 512, SETS * ja),)
+            if blocks[-1] == blocks[0] + len(blocks) - 1:
+                parts = ((0, width, SETS * blocks[0]),)
             else:
-                parts = ((0, SETS, SETS * ja), (SETS, SETS, SETS * jb))
+                parts = tuple((SETS * q, SETS, SETS * blocks[q]) for q in range(2))
             for t in range(4):
                 x = ps_x.tile([P, 512], F32, tag="x")
-                for o0, width, c0 in parts:
+                for o0, part, c0 in parts:
                     nc.tensor.matmul_mx(
-                        out=x[:, o0 : o0 + width],
+                        out=x[:, o0 : o0 + part],
                         lhsT=w1_codes[swap][:, P * t : P * t + P].bitcast(FP8X4),
                         lhsT_scale=w1_scales[swap][:, P * t : P * t + P],
-                        rhs=rot_codes[r][:, c0 : c0 + width].bitcast(FP8X4),
-                        rhs_scale=rot_scales[r][:, c0 : c0 + width],
+                        rhs=rot_codes[r][:, c0 : c0 + part].bitcast(FP8X4),
+                        rhs_scale=rot_scales[r][:, c0 : c0 + part],
                         start=True,
                         stop=True,
                     )
-                if i == n - 1 and t % 2 == 1:
+                if i == 0 and t == 3:
                     nc.vector.tensor_scalar(
-                        out=hid[:, t, :], in0=x[:], scalar1=b1_f[:, t : t + 1], scalar2=0.0, op0=ALU.add, op1=ALU.max
+                        out=hid[:, t, :width], in0=x[:, :width], scalar1=b1_f[:, t : t + 1], scalar2=0.0, op0=ALU.add, op1=ALU.max
                     )
                 else:
-                    nc.scalar.activation(out=hid[:, t, :], in_=x[:], func=ACT.Relu, bias=b1_f[:, t : t + 1], scale=1.0)
+                    nc.scalar.activation(out=hid[:, t, :width], in_=x[:, :width], func=ACT.Relu, bias=b1_f[:, t : t + 1], scale=1.0)
             st[("hid", i)] = hid
 
         def regroup(i):
             hid = st[("hid", i)]
+            width = SETS * len(chunks[i][2])
             grp = work.tile([P, 512, 4], BF16, tag="grp", align_bytes=64)
             nc.vector.tensor_copy(
-                out=grp[:].rearrange("p (c i) t -> p c t i", i=4),
-                in_=hid[:].rearrange("p t (c i) -> p c t i", i=4),
+                out=grp[:, :width, :].rearrange("p (c i) t -> p c t i", i=4),
+                in_=hid[:, :, :width].rearrange("p t (c i) -> p c t i", i=4),
             )
             st[("grp", i)] = grp
 
         def quantise(i):
             grp = st[("grp", i)]
+            width = SETS * len(chunks[i][2])
             hc = work.tile([P, 512], U32, tag="hc", align_bytes=64)
             hs = work.tile([P, 512], U8, tag="hs", align_bytes=64)
-            nc.vector.quantize_mx(out=hc[:].bitcast(FP8X4), scales=hs[:], in_=grp[:].rearrange("p w t -> p (w t)"))
+            nc.vector.quantize_mx(
+                out=hc[:, :width].bitcast(FP8X4),
+                scales=hs[:, :width],
+                in_=grp[:].rearrange("p w t -> p (w t)")[:, : 4 * width],
+            )
             st[("h", i)] = (hc, hs)
 
         def layer2(i):
             hc, hs = st[("h", i)]
+            count = len(chunks[i][2])
             y = ps_y.tile([P, 4, P], F32, tag="y")
             for h in range(2):
-                for q in range(2):
+                for q in range(count):
                     c0 = SETS * q + P * h
                     nc.tensor.matmul_mx(
-                        out=y[:, 2 * h + q, :],
+                        out=y[:, count * h + q, :],
                         lhsT=hc[:, c0 : c0 + P].bitcast(FP8X4),
                         lhsT_scale=hs[:, c0 : c0 + P],
                         rhs=w2_codes[:].bitcast(FP8X4),
@@ -229,11 +239,12 @@ def tile_pairwiserelationmodule_pa_t_kernel(tc, objs, W1, b1, W2, b2, out_0, out
 
         def bias2(i):
             y = st[("y", i)]
+            slots = 2 * len(chunks[i][2])
             z = work.tile([P, 512], F32, tag="z")
             nc.vector.tensor_tensor(
-                out=z[:].rearrange("p (j g) -> p j g", g=P),
-                in0=y[:],
-                in1=b2_f[:].unsqueeze(1).to_broadcast([P, 4, P]),
+                out=z[:, : slots * P].rearrange("p (j g) -> p j g", g=P),
+                in0=y[:, :slots, :],
+                in1=b2_f[:].unsqueeze(1).to_broadcast([P, slots, P]),
                 op=ALU.add,
             )
             st[("z", i)] = z
@@ -241,13 +252,15 @@ def tile_pairwiserelationmodule_pa_t_kernel(tc, objs, W1, b1, W2, b2, out_0, out
         def finish(i):
             r, swap, blocks = chunks[i]
             z = st[("z", i)]
+            count = len(blocks)
+            width = SETS * count
             xo = outp.tile([P, 512], F32, tag="xo")
             if i % RELU_ON_VECTOR_EVERY == 0 and i < n - 4:
-                nc.vector.tensor_scalar_max(out=xo[:], in0=z[:], scalar1=0.0)
+                nc.vector.tensor_scalar_max(out=xo[:, :width], in0=z[:, :width], scalar1=0.0)
             else:
-                nc.scalar.activation(out=xo[:], in_=z[:], func=ACT.Relu)
-            xo_v = xo[:].rearrange("p (h q g) -> p h q g", h=2, q=2)
-            for q in range(2):
+                nc.scalar.activation(out=xo[:, :width], in_=z[:, :width], func=ACT.Relu)
+            xo_v = xo[:, :width].rearrange("p (h q g) -> p h q g", h=2, q=count)
+            for q in range(count):
                 top = blocks[q]
                 bot = (top + r) % OBJ
                 m, k = (top, bot) if swap == 0 else (bot, top)
@@ -264,35 +277,62 @@ def tile_pairwiserelationmodule_pa_t_kernel(tc, objs, W1, b1, W2, b2, out_0, out
                         lhsT=xo[:, c0 : c0 + P],
                         rhs=ident[:],
                         start=(i == 0 and q == 0),
-                        stop=(i == n - 1 and q == 1),
+                        stop=(i == n - 3 and q == 1),
                         is_transpose=True,
                     )
 
+        def prepare_w2():
+            p2 = ps_y.tile([P, 4, P], F32, tag="y")
+            for u in range(2):
+                nc.tensor.transpose(p2[:, u, :], w2_words[:, :, u], ident[:])
+            copy_out("s", w2_grp[:].bitcast(F32).rearrange("p (c u) -> p c u", u=2), p2[:, 0:2, :].rearrange("p u c -> p c u"))
+
+        def quantise_w2():
+            nc.vector.quantize_mx(out=w2_codes[:].bitcast(FP8X4), scales=w2_scales[:], in_=w2_grp[:])
+            nc.vector.tensor_copy(out=b2_f[:], in_=b2_raw[:])
+
+        sum_sb = keep.tile([P, 2, P], F32)
+        partial = keep.tile([P, 2, P], F32)
+        total = keep.tile([P, 2, P], F32)
+
+        def turn_sums_back():
+            nc.vector.tensor_copy(out=sum_sb[:, 0, :], in_=sum_t[0][:])
+            nc.scalar.copy(out=sum_sb[:, 1, :], in_=sum_t[1][:])
+            back = ps_x.tile([P, 4, P], F32, tag="x")
+            for h in range(2):
+                nc.tensor.transpose(back[:, h, :], sum_sb[:, h, :], ident[:])
+            st["back"] = back
+
+        def add_last(out, so_far, i):
+            xo = st[("xo", i)]
+            nc.vector.tensor_tensor(
+                out=out[:], in0=so_far, in1=xo[:, :SETS].rearrange("p (h g) -> p h g", g=P), op=ALU.add
+            )
+
         rotate_at = {0: 2, 6: 3, 12: 4, 17: 0}
-        for i in range(n + 7):
+        for i in range(n + 5):
             if i in rotate_at:
                 make_rotated(rotate_at[i])
             if i < n:
                 layer1(i)
+            if i == 1:
+                prepare_w2()
+            if i == 2:
+                quantise_w2()
             if 0 <= i - 3 < n:
                 layer2(i - 3)
-            if 0 <= i - 6 < n:
-                add_up(i - 6)
+            if 0 <= i - 5 < n - 2:
+                add_up(i - 5)
             if 0 <= i - 1 < n:
                 regroup(i - 1)
-            if 0 <= i - 4 < n:
-                bias2(i - 4)
+            if 0 <= i - 3 < n:
+                bias2(i - 3)
             if 0 <= i - 1 < n:
                 quantise(i - 1)
-            if 0 <= i - 5 < n:
-                finish(i - 5)
-
-        sum_sb = keep.tile([P, 2, P], F32)
-        nc.vector.tensor_copy(out=sum_sb[:, 0, :], in_=sum_t[0][:])
-        nc.scalar.copy(out=sum_sb[:, 1, :], in_=sum_t[1][:])
-        back = ps_y.tile([P, 4, P], F32, tag="y")
-        for h in range(2):
-            nc.tensor.transpose(back[:, h, :], sum_sb[:, h, :], ident[:])
-        total = keep.tile([P, 2, P], F32)
-        nc.vector.tensor_copy(out=total[:], in_=back[:, 0:2, :])
+            if i == n + 3:
+                turn_sums_back()
+            if 0 <= i - 4 < n:
+                finish(i - 4)
+        add_last(partial, st["back"][:, 0:2, :], n - 2)
+        add_last(total, partial[:], n - 1)
         nc.sync.dma_start(out=out_1.rearrange("(h p) g -> p h g", p=P), in_=total[:])

@@ -31,21 +31,32 @@ def tile_pairwiserelationmodule_pa_t_kernel(tc, objs, W1, b1, W2, b2, out_0, out
         ps_s = ctx.enter_context(tc.psum_pool(name="ps_s", bufs=1))
         ctx.enter_context(tc.manual_schedule())
 
-        w1_raw = keep.tile([P, 4 * 512], BF16)
-        nc.sync.dma_start(out=w1_raw[:], in_=W1.rearrange("(p t) k -> p (t k)", t=4))
+        w1_rows = W1.rearrange("(p t) k -> p t k", t=4)
+        w1_raw0 = keep.tile([P, 2, 512], BF16)
+        w1_raw1 = keep.tile([P, 2, 512], BF16)
+        w1_raw = [w1_raw0, w1_raw1]
         obj_rows = objs.rearrange("(h p) o d -> h p (o d)", p=P)
         obj_raw00 = keep.tile([P, 1024], BF16)
         obj_raw01 = keep.tile([P, 1024], BF16)
         obj_raw10 = keep.tile([P, 1024], BF16)
         obj_raw11 = keep.tile([P, 1024], BF16)
         obj_raw = [[obj_raw00, obj_raw01], [obj_raw10, obj_raw11]]
-        for half in range(2):
+        b1_raw = keep.tile([P, 4], BF16)
+
+        def load_w1(half):
+            nc.sync.dma_start(out=w1_raw[half][:], in_=w1_rows[:, 2 * half : 2 * half + 2, :])
+
+        def load_objects(half):
             for h in range(2):
                 nc.sync.dma_start(out=obj_raw[half][h][:], in_=obj_rows[h, :, 1024 * half : 1024 * half + 1024])
+
+        load_w1(0)
+        load_objects(0)
+        load_w1(1)
+        nc.sync.dma_start(out=b1_raw[:], in_=b1.rearrange("(p t) -> p t", t=4))
+        load_objects(1)
         w2_raw = keep.tile([P, 512], BF16)
         nc.sync.dma_start(out=w2_raw[:], in_=W2)
-        b1_raw = keep.tile([P, 4], BF16)
-        nc.sync.dma_start(out=b1_raw[:], in_=b1.rearrange("(p t) -> p t", t=4))
         b2_raw = keep.tile([P, P], BF16)
         nc.sync.dma_start(out=b2_raw[:], in_=b2.partition_broadcast(P))
 
@@ -69,7 +80,10 @@ def tile_pairwiserelationmodule_pa_t_kernel(tc, objs, W1, b1, W2, b2, out_0, out
 
         w1_grp = keep.tile([P, 4 * P * 4], BF16, align_bytes=64)
         w1_grp_v = w1_grp[:].bitcast(F32).rearrange("p (t c u) -> p t c u", t=4, u=2)
-        w1_words = w1_raw[:].bitcast(F32).rearrange("p (t c u) -> p t c u", t=4, u=2)
+        w1_words = [
+            w1_raw[half][:].rearrange("p t k -> p (t k)").bitcast(F32).rearrange("p (t c u) -> p t c u", t=2, u=2)
+            for half in range(2)
+        ]
         obj_grp = keep.tile([P, 4 * SETS * 4], BF16, align_bytes=64)
         obj_grp_v = obj_grp[:].bitcast(F32).rearrange("p (s h c u) -> p s h c u", s=4, h=2, u=2)
         obj_words = [
@@ -96,38 +110,62 @@ def tile_pairwiserelationmodule_pa_t_kernel(tc, objs, W1, b1, W2, b2, out_0, out
                 in_=obj_grp[:, 1024 * s : 1024 * s + 1024],
             )
 
-        w1_banks = []
-        for t0 in (0, 2):
-            pw = ps_x.tile([P, 4, P], F32, tag="x")
-            for dt in range(2):
+        def w1_transposes(half):
+            bank = ps_x.tile([P, 4, P], F32, tag="x")
+            for t in range(2):
                 for u in range(2):
-                    nc.tensor.transpose(pw[:, 2 * dt + u, :], w1_words[:, t0 + dt, :, u], ident[:])
-            w1_banks.append(pw)
-        obj_banks = []
-        for s in range(4):
-            if s < 2:
-                po = ps_x.tile([P, 4, P], F32, tag="x")
-            else:
-                po = ps_y.tile([P, 4, P], F32, tag="y")
-            for h in range(2):
+                    nc.tensor.transpose(bank[:, 2 * t + u, :], w1_words[half][:, t, :, u], ident[:])
+            return bank
+
+        def w1_copy(half, engine, bank):
+            copy_out(
+                engine, w1_grp_v[:, 2 * half : 2 * half + 2], bank[:].rearrange("p (t u) c -> p t c u", u=2)
+            )
+
+        def w1_quantise(half):
+            cols = slice(2 * P * half, 2 * P * half + 2 * P)
+            nc.vector.quantize_mx(
+                out=w1_codes0[:, cols].bitcast(FP8X4),
+                scales=w1_scales0[:, cols],
+                in_=w1_grp[:, 1024 * half : 1024 * half + 1024],
+            )
+
+        def object_transposes(half, h, bank):
+            for s in range(2):
                 for u in range(2):
-                    nc.tensor.transpose(po[:, 2 * h + u, :], obj_words[s // 2][h][:, s % 2, :, u], ident[:])
-            obj_banks.append(po)
-        for which, engine in ((0, "v"), (1, "s")):
-            copy_out(engine, w1_grp_v[:, 2 * which : 2 * which + 2], w1_banks[which][:].rearrange("p (t u) c -> p t c u", u=2))
-        for s, engine in ((0, "v"), (1, "s")):
-            copy_out(engine, obj_grp_v[:, s], obj_banks[s][:].rearrange("p (h u) c -> p h c u", u=2))
-        nc.vector.quantize_mx(out=w1_codes0[:].bitcast(FP8X4), scales=w1_scales0[:], in_=w1_grp[:])
+                    nc.tensor.transpose(bank[:, 2 * s + u, :], obj_words[half][h][:, s, :, u], ident[:])
+
+        def object_copy(half, h, engine, bank):
+            copy_out(
+                engine, obj_grp_v[:, 2 * half : 2 * half + 2, h], bank[:].rearrange("p (s u) c -> p s c u", u=2)
+            )
+
+        w1_bank0 = w1_transposes(0)
+        obj_bank00 = ps_x.tile([P, 4, P], F32, tag="x")
+        object_transposes(0, 0, obj_bank00)
+        obj_bank01 = ps_x.tile([P, 4, P], F32, tag="x")
+        object_transposes(0, 1, obj_bank01)
+        w1_bank1 = w1_transposes(1)
+        obj_bank10 = ps_y.tile([P, 4, P], F32, tag="y")
+        object_transposes(1, 0, obj_bank10)
+        obj_bank11 = ps_y.tile([P, 4, P], F32, tag="y")
+        object_transposes(1, 1, obj_bank11)
+        w1_copy(0, "v", w1_bank0)
+        object_copy(0, 0, "s", obj_bank00)
+        w1_quantise(0)
+        object_copy(0, 1, "v", obj_bank01)
+        w1_copy(1, "s", w1_bank1)
+        obj_quantise(0)
+        obj_quantise(1)
+        nc.vector.tensor_copy(out=b1_f[:], in_=b1_raw[:])
+        w1_quantise(1)
         for dst_t, src_t in ((w1_codes1, w1_codes0), (w1_scales1, w1_scales0)):
             dv = dst_t[:].bitcast(I32)
             sv = src_t[:].bitcast(I32)
             nc.sync.dma_start(out=dv[0:64, :], in_=sv[64:128, :])
             nc.sync.dma_start(out=dv[64:128, :], in_=sv[0:64, :])
-        obj_quantise(0)
-        obj_quantise(1)
-        nc.vector.tensor_copy(out=b1_f[:], in_=b1_raw[:])
-        for s, engine in ((2, "v"), (3, "s")):
-            copy_out(engine, obj_grp_v[:, s], obj_banks[s][:].rearrange("p (h u) c -> p h c u", u=2))
+        object_copy(1, 0, "s", obj_bank10)
+        object_copy(1, 1, "v", obj_bank11)
         obj_quantise(2)
         obj_quantise(3)
         for t_ in (codes1, scales1):
@@ -277,7 +315,7 @@ def tile_pairwiserelationmodule_pa_t_kernel(tc, objs, W1, b1, W2, b2, out_0, out
                         lhsT=xo[:, c0 : c0 + P],
                         rhs=ident[:],
                         start=(i == 0 and q == 0),
-                        stop=(i == n - 3 and q == 1),
+                        stop=(i == n - 4 and q == 1),
                         is_transpose=True,
                     )
 
@@ -292,47 +330,61 @@ def tile_pairwiserelationmodule_pa_t_kernel(tc, objs, W1, b1, W2, b2, out_0, out
             nc.vector.tensor_copy(out=b2_f[:], in_=b2_raw[:])
 
         sum_sb = keep.tile([P, 2, P], F32)
-        partial = keep.tile([P, 2, P], F32)
-        total = keep.tile([P, 2, P], F32)
 
         def turn_sums_back():
-            nc.vector.tensor_copy(out=sum_sb[:, 0, :], in_=sum_t[0][:])
-            nc.scalar.copy(out=sum_sb[:, 1, :], in_=sum_t[1][:])
             back = ps_x.tile([P, 4, P], F32, tag="x")
             for h in range(2):
                 nc.tensor.transpose(back[:, h, :], sum_sb[:, h, :], ident[:])
             st["back"] = back
 
-        def add_last(out, so_far, i):
-            xo = st[("xo", i)]
-            nc.vector.tensor_tensor(
-                out=out[:], in0=so_far, in1=xo[:, :SETS].rearrange("p (h g) -> p h g", g=P), op=ALU.add
-            )
+        def add_to_sums(so_far, part):
+            sums = work.tile([P, 2, P], F32, tag="sums")
+            nc.vector.tensor_tensor(out=sums[:], in0=so_far, in1=part, op=ALU.add)
+            return sums
 
         rotate_at = {0: 2, 6: 3, 12: 4, 17: 0}
-        for i in range(n + 5):
+        for i in range(n):
             if i in rotate_at:
                 make_rotated(rotate_at[i])
-            if i < n:
-                layer1(i)
+            layer1(i)
             if i == 1:
                 prepare_w2()
             if i == 2:
                 quantise_w2()
-            if 0 <= i - 3 < n:
+            if i >= 3:
                 layer2(i - 3)
-            if 0 <= i - 5 < n - 2:
+            if i >= 5:
                 add_up(i - 5)
-            if 0 <= i - 1 < n:
+            if i >= 1:
                 regroup(i - 1)
-            if 0 <= i - 3 < n:
+            if i >= 3:
                 bias2(i - 3)
-            if 0 <= i - 1 < n:
+            if i >= 1:
                 quantise(i - 1)
-            if i == n + 3:
-                turn_sums_back()
-            if 0 <= i - 4 < n:
+            if i >= 4:
                 finish(i - 4)
-        add_last(partial, st["back"][:, 0:2, :], n - 2)
-        add_last(total, partial[:], n - 1)
+
+        layer2(n - 3)
+        add_up(n - 5)
+        regroup(n - 1)
+        bias2(n - 3)
+        quantise(n - 1)
+        finish(n - 4)
+        layer2(n - 2)
+        add_up(n - 4)
+        bias2(n - 2)
+        nc.scalar.copy(out=sum_sb[:, 0, :], in_=sum_t[0][:])
+        nc.vector.tensor_copy(out=sum_sb[:, 1, :], in_=sum_t[1][:])
+        finish(n - 3)
+        layer2(n - 1)
+        turn_sums_back()
+        bias2(n - 1)
+        finish(n - 2)
+        finish(n - 1)
+        xo_v = st[("xo", n - 3)][:].rearrange("p (h q g) -> p h q g", h=2, q=2)
+        early = add_to_sums(st["back"][:, 0:2, :], xo_v[:, :, 0, :])
+        late = xo_v[:, :, 1, :]
+        for i in (n - 2, n - 1):
+            late = add_to_sums(late, st[("xo", i)][:, :SETS].rearrange("p (h g) -> p h g", g=P))[:]
+        total = add_to_sums(early[:], late)
         nc.sync.dma_start(out=out_1.rearrange("(h p) g -> p h g", p=P), in_=total[:])

@@ -31,6 +31,16 @@ def tile_pairwiserelationmodule_pa_t_kernel(tc, objs, W1, b1, W2, b2, out_0, out
         ps_s = ctx.enter_context(tc.psum_pool(name="ps_s", bufs=1))
         ctx.enter_context(tc.manual_schedule())
 
+        zeros = keep.tile([P, 512], BF16)
+        nc.vector.memset(zeros[:].bitcast(I32), 0)
+        idle_bank = ps_x.tile([P, 512], F32, tag="x")
+
+        def keep_busy(count):
+            for repeat in range(count):
+                nc.tensor.matmul(out=idle_bank[:], lhsT=zeros[:, 0:P], rhs=zeros[:], start=True, stop=True)
+
+        keep_busy(4)
+
         w1_rows = W1.rearrange("(p t) k -> p t k", t=4)
         w1_raw0 = keep.tile([P, 2, 512], BF16)
         w1_raw1 = keep.tile([P, 2, 512], BF16)
@@ -293,7 +303,7 @@ def tile_pairwiserelationmodule_pa_t_kernel(tc, objs, W1, b1, W2, b2, out_0, out
             count = len(blocks)
             width = SETS * count
             xo = outp.tile([P, 512], F32, tag="xo")
-            if i % RELU_ON_VECTOR_EVERY == 0 and i < n - 4:
+            if i % RELU_ON_VECTOR_EVERY == 0 and i < n - 5:
                 nc.vector.tensor_scalar_max(out=xo[:, :width], in0=z[:, :width], scalar1=0.0)
             else:
                 nc.scalar.activation(out=xo[:, :width], in_=z[:, :width], func=ACT.Relu)
@@ -365,12 +375,12 @@ def tile_pairwiserelationmodule_pa_t_kernel(tc, objs, W1, b1, W2, b2, out_0, out
                 finish(i - 4)
 
         layer2(n - 3)
-        add_up(n - 5)
         regroup(n - 1)
         bias2(n - 3)
         quantise(n - 1)
         finish(n - 4)
         layer2(n - 2)
+        add_up(n - 5)
         add_up(n - 4)
         bias2(n - 2)
         nc.scalar.copy(out=sum_sb[:, 0, :], in_=sum_t[0][:])

@@ -16,7 +16,6 @@ P = 128
 SETS = 256
 OBJ = 8
 FLOPS = 2 * SETS * OBJ * OBJ * 512 * (512 + 128)
-RELU_ON_VECTOR_EVERY = 2
 
 
 def tile_pairwiserelationmodule_pa_t_kernel(tc, objs, W1, b1, W2, b2, out_0, out_1):
@@ -33,9 +32,9 @@ def tile_pairwiserelationmodule_pa_t_kernel(tc, objs, W1, b1, W2, b2, out_0, out
 
         zeros = keep.tile([P, 512], BF16)
         nc.vector.memset(zeros[:].bitcast(I32), 0)
-        idle_bank = ps_x.tile([P, 512], F32, tag="x")
 
         def keep_busy(count):
+            idle_bank = ps_x.tile([P, 512], F32, tag="x")
             for repeat in range(count):
                 nc.tensor.matmul(out=idle_bank[:], lhsT=zeros[:, 0:P], rhs=zeros[:], start=True, stop=True)
 
@@ -69,6 +68,9 @@ def tile_pairwiserelationmodule_pa_t_kernel(tc, objs, W1, b1, W2, b2, out_0, out
         nc.sync.dma_start(out=w2_raw[:], in_=W2)
         b2_raw = keep.tile([P, P], BF16)
         nc.sync.dma_start(out=b2_raw[:], in_=b2.partition_broadcast(P))
+        b2_col_raw = keep.tile([P, 1], BF16)
+        nc.sync.dma_start(out=b2_col_raw[:], in_=b2.rearrange("(p o) -> p o", o=1))
+        b2_col = keep.tile([P, 1], F32)
 
         ident = keep.tile([P, P], F32)
         make_identity(nc, ident[:])
@@ -245,13 +247,14 @@ def tile_pairwiserelationmodule_pa_t_kernel(tc, objs, W1, b1, W2, b2, out_0, out
                     nc.scalar.activation(out=hid[:, t, :width], in_=x[:, :width], func=ACT.Relu, bias=b1_f[:, t : t + 1], scale=1.0)
             st[("hid", i)] = hid
 
-        def regroup(i):
+        def regroup(i, engine="v"):
             hid = st[("hid", i)]
             width = SETS * len(chunks[i][2])
             grp = work.tile([P, 512, 4], BF16, tag="grp", align_bytes=64)
-            nc.vector.tensor_copy(
-                out=grp[:, :width, :].rearrange("p (c i) t -> p c t i", i=4),
-                in_=hid[:, :, :width].rearrange("p t (c i) -> p c t i", i=4),
+            copy_out(
+                engine,
+                grp[:, :width, :].rearrange("p (c i) t -> p c t i", i=4),
+                hid[:, :, :width].rearrange("p t (c i) -> p c t i", i=4),
             )
             st[("grp", i)] = grp
 
@@ -285,6 +288,39 @@ def tile_pairwiserelationmodule_pa_t_kernel(tc, objs, W1, b1, W2, b2, out_0, out
                     )
             st[("y", i)] = y
 
+        def is_turned(i):
+            return i % 5 == 2 and i < n - 5
+
+        def layer2_turned(i):
+            hc, hs = st[("h", i)]
+            y = ps_y.tile([P, 4, P], F32, tag="y")
+            nc.tensor.matmul_mx(
+                out=y[:].rearrange("p j c -> p (j c)"),
+                lhsT=w2_codes[:].bitcast(FP8X4),
+                lhsT_scale=w2_scales[:],
+                rhs=hc[:].bitcast(FP8X4),
+                rhs_scale=hs[:],
+                start=True,
+                stop=True,
+            )
+            st[("y", i)] = y
+
+        def relu_turned(i):
+            turned = work.tile([P, 512], F32, tag="turned")
+            nc.scalar.activation(
+                out=turned[:], in_=st[("y", i)][:].rearrange("p j c -> p (j c)"), func=ACT.Relu, bias=b2_col[:], scale=1.0
+            )
+            st[("turned", i)] = turned
+
+        def turn_back(i):
+            turned = st[("turned", i)]
+            z = ps_y.tile([P, 4, P], F32, tag="y")
+            for h in range(2):
+                for q in range(2):
+                    c0 = SETS * q + P * h
+                    nc.tensor.transpose(z[:, 2 * h + q, :], turned[:, c0 : c0 + P], ident[:])
+            st[("z", i)] = z
+
         def bias2(i):
             y = st[("y", i)]
             slots = 2 * len(chunks[i][2])
@@ -303,7 +339,9 @@ def tile_pairwiserelationmodule_pa_t_kernel(tc, objs, W1, b1, W2, b2, out_0, out
             count = len(blocks)
             width = SETS * count
             xo = outp.tile([P, 512], F32, tag="xo")
-            if i % RELU_ON_VECTOR_EVERY == 0 and i < n - 5:
+            if is_turned(i):
+                nc.scalar.copy(out=xo[:], in_=z[:].rearrange("p j g -> p (j g)"))
+            elif i < n - 5:
                 nc.vector.tensor_scalar_max(out=xo[:, :width], in0=z[:, :width], scalar1=0.0)
             else:
                 nc.scalar.activation(out=xo[:, :width], in_=z[:, :width], func=ACT.Relu)
@@ -338,6 +376,7 @@ def tile_pairwiserelationmodule_pa_t_kernel(tc, objs, W1, b1, W2, b2, out_0, out
         def quantise_w2():
             nc.vector.quantize_mx(out=w2_codes[:].bitcast(FP8X4), scales=w2_scales[:], in_=w2_grp[:])
             nc.vector.tensor_copy(out=b2_f[:], in_=b2_raw[:])
+            nc.vector.tensor_copy(out=b2_col[:], in_=b2_col_raw[:])
 
         sum_sb = keep.tile([P, 2, P], F32)
 
@@ -347,9 +386,13 @@ def tile_pairwiserelationmodule_pa_t_kernel(tc, objs, W1, b1, W2, b2, out_0, out
                 nc.tensor.transpose(back[:, h, :], sum_sb[:, h, :], ident[:])
             st["back"] = back
 
-        def add_to_sums(so_far, part):
+        def add_to_sums(part, i=None, so_far=None):
             sums = work.tile([P, 2, P], F32, tag="sums")
-            nc.vector.tensor_tensor(out=sums[:], in0=so_far, in1=part, op=ALU.add)
+            if i is None:
+                nc.vector.tensor_tensor(out=sums[:], in0=part, in1=so_far, op=ALU.add)
+            else:
+                z_v = st[("z", i)][:, :SETS].rearrange("p (h g) -> p h g", g=P)
+                nc.vector.scalar_tensor_tensor(out=sums[:], in0=z_v, scalar=0.0, in1=part, op0=ALU.max, op1=ALU.add)
             return sums
 
         rotate_at = {0: 2, 6: 3, 12: 4, 17: 0}
@@ -357,44 +400,54 @@ def tile_pairwiserelationmodule_pa_t_kernel(tc, objs, W1, b1, W2, b2, out_0, out
             if i in rotate_at:
                 make_rotated(rotate_at[i])
             layer1(i)
+            if i == n - 1:
+                regroup(i, "s")
             if i == 1:
                 prepare_w2()
             if i == 2:
                 quantise_w2()
-            if i >= 3:
+            if i >= 3 and is_turned(i - 3):
+                layer2_turned(i - 3)
+                relu_turned(i - 3)
+            elif i >= 3:
                 layer2(i - 3)
+            if i >= 4 and is_turned(i - 4):
+                turn_back(i - 4)
             if i >= 5:
                 add_up(i - 5)
             if i >= 1:
                 regroup(i - 1)
-            if i >= 3:
+            if i >= 3 and not is_turned(i - 3):
                 bias2(i - 3)
-            if i >= 1:
-                quantise(i - 1)
-            if i >= 4:
+            if i >= 3 and is_turned(i - 3):
                 finish(i - 4)
+                quantise(i - 1)
+            else:
+                if i >= 1:
+                    quantise(i - 1)
+                if i >= 4:
+                    finish(i - 4)
 
         layer2(n - 3)
-        regroup(n - 1)
+        keep_busy(3)
         bias2(n - 3)
         quantise(n - 1)
         finish(n - 4)
         layer2(n - 2)
+        layer2(n - 1)
         add_up(n - 5)
         add_up(n - 4)
         bias2(n - 2)
-        nc.scalar.copy(out=sum_sb[:, 0, :], in_=sum_t[0][:])
-        nc.vector.tensor_copy(out=sum_sb[:, 1, :], in_=sum_t[1][:])
         finish(n - 3)
-        layer2(n - 1)
-        turn_sums_back()
         bias2(n - 1)
         finish(n - 2)
         finish(n - 1)
         xo_v = st[("xo", n - 3)][:].rearrange("p (h q g) -> p h q g", h=2, q=2)
-        early = add_to_sums(st["back"][:, 0:2, :], xo_v[:, :, 0, :])
-        late = xo_v[:, :, 1, :]
-        for i in (n - 2, n - 1):
-            late = add_to_sums(late, st[("xo", i)][:, :SETS].rearrange("p (h g) -> p h g", g=P))[:]
-        total = add_to_sums(early[:], late)
+        first = add_to_sums(xo_v[:, :, 0, :], i=n - 2)
+        second = add_to_sums(xo_v[:, :, 1, :], i=n - 1)
+        for h in range(2):
+            nc.vector.tensor_copy(out=sum_sb[:, h, :], in_=sum_t[h][:])
+        turn_sums_back()
+        both = add_to_sums(first[:], so_far=second[:])
+        total = add_to_sums(st["back"][:, 0:2, :], so_far=both[:])
         nc.sync.dma_start(out=out_1.rearrange("(h p) g -> p h g", p=P), in_=total[:])

@@ -25,7 +25,7 @@ def tile_pairwiserelationmodule_pa_t_kernel(tc, objs, W1, b1, W2, b2, out_0, out
         work = ctx.enter_context(tc.tile_pool(name="work", bufs=4))
         outp = ctx.enter_context(tc.tile_pool(name="outp", bufs=8))
         rotp = ctx.enter_context(tc.tile_pool(name="rotp", bufs=3))
-        ps_x = ctx.enter_context(tc.psum_pool(name="ps_x", bufs=4))
+        ps_x = ctx.enter_context(tc.psum_pool(name="ps_x", bufs=5))
         ps_y = ctx.enter_context(tc.psum_pool(name="ps_y", bufs=2))
         ps_s = ctx.enter_context(tc.psum_pool(name="ps_s", bufs=1))
         ctx.enter_context(tc.manual_schedule())
@@ -141,6 +141,11 @@ def tile_pairwiserelationmodule_pa_t_kernel(tc, objs, W1, b1, W2, b2, out_0, out
                 scales=w1_scales0[:, cols],
                 in_=w1_grp[:, 1024 * half : 1024 * half + 1024],
             )
+            for dst_t, src_t in ((w1_codes1, w1_codes0), (w1_scales1, w1_scales0)):
+                dv = dst_t[:, cols].bitcast(I32)
+                sv = src_t[:, cols].bitcast(I32)
+                nc.sync.dma_start(out=dv[0:64, :], in_=sv[64:128, :])
+                nc.sync.dma_start(out=dv[64:128, :], in_=sv[0:64, :])
 
         def object_transposes(half, h, bank):
             for s in range(2):
@@ -171,11 +176,6 @@ def tile_pairwiserelationmodule_pa_t_kernel(tc, objs, W1, b1, W2, b2, out_0, out
         obj_quantise(1)
         nc.vector.tensor_copy(out=b1_f[:], in_=b1_raw[:])
         w1_quantise(1)
-        for dst_t, src_t in ((w1_codes1, w1_codes0), (w1_scales1, w1_scales0)):
-            dv = dst_t[:].bitcast(I32)
-            sv = src_t[:].bitcast(I32)
-            nc.sync.dma_start(out=dv[0:64, :], in_=sv[64:128, :])
-            nc.sync.dma_start(out=dv[64:128, :], in_=sv[0:64, :])
         object_copy(1, 0, "s", obj_bank10)
         object_copy(1, 1, "v", obj_bank11)
         obj_quantise(2)
@@ -200,9 +200,7 @@ def tile_pairwiserelationmodule_pa_t_kernel(tc, objs, W1, b1, W2, b2, out_0, out
                 nc.sync.dma_start(out=dv[64:128, cut : OBJ * w], in_=sv[64:128, 0 : shift * w])
 
         out_rows = out_0.rearrange("(h p) q g -> p h q g", p=P)
-        sum_t0 = ps_s.tile([P, P], F32)
-        sum_t1 = ps_s.tile([P, P], F32)
-        sum_t = [sum_t0, sum_t1]
+        sum_t = ps_s.tile([P, 2, P], F32)
 
         chunks = []
         for blocks in (((0, 2), (4, 6)), ((1, 3), (5, 7))):
@@ -359,11 +357,11 @@ def tile_pairwiserelationmodule_pa_t_kernel(tc, objs, W1, b1, W2, b2, out_0, out
                 for q in range(2):
                     c0 = (2 * h + q) * P
                     nc.tensor.matmul(
-                        out=sum_t[h][:],
+                        out=sum_t[:, h, :],
                         lhsT=xo[:, c0 : c0 + P],
                         rhs=ident[:],
-                        start=(i == 0 and q == 0),
-                        stop=(i == n - 4 and q == 1),
+                        start=(i == 0 and h == 0 and q == 0),
+                        stop=(i == n - 4 and h == 1 and q == 1),
                         is_transpose=True,
                     )
 
@@ -440,13 +438,12 @@ def tile_pairwiserelationmodule_pa_t_kernel(tc, objs, W1, b1, W2, b2, out_0, out
         bias2(n - 2)
         finish(n - 3)
         bias2(n - 1)
+        nc.scalar.copy(out=sum_sb[:], in_=sum_t[:])
         finish(n - 2)
         finish(n - 1)
         xo_v = st[("xo", n - 3)][:].rearrange("p (h q g) -> p h q g", h=2, q=2)
         first = add_to_sums(xo_v[:, :, 0, :], i=n - 2)
         second = add_to_sums(xo_v[:, :, 1, :], i=n - 1)
-        for h in range(2):
-            nc.vector.tensor_copy(out=sum_sb[:, h, :], in_=sum_t[h][:])
         turn_sums_back()
         both = add_to_sums(first[:], so_far=second[:])
         total = add_to_sums(st["back"][:, 0:2, :], so_far=both[:])

from contextlib import ExitStack

import concourse.mybir as mybir
from concourse.masks import make_identity

F32 = mybir.dt.float32
BF16 = mybir.dt.bfloat16
U32 = mybir.dt.uint32
I32 = mybir.dt.int32
U8 = mybir.dt.uint8
FP8X4 = mybir.dt.float8_e4m3fn_x4
ACT = mybir.ActivationFunctionType
ALU = mybir.AluOpType

P = 128
SETS = 256
OBJ = 8
FLOPS = 2 * SETS * OBJ * OBJ * 512 * (512 + 128)


def tile_pairwiserelationmodule_pa_t_kernel(tc, objs, W1, b1, W2, b2, out_0, out_1):
    nc = tc.nc
    with ExitStack() as ctx:
        keep = ctx.enter_context(tc.tile_pool(name="keep", bufs=1))
        work = ctx.enter_context(tc.tile_pool(name="work", bufs=4))
        outp = ctx.enter_context(tc.tile_pool(name="outp", bufs=8))
        rotp = ctx.enter_context(tc.tile_pool(name="rotp", bufs=3))
        ps_x = ctx.enter_context(tc.psum_pool(name="ps_x", bufs=5))
        ps_y = ctx.enter_context(tc.psum_pool(name="ps_y", bufs=2))
        ps_s = ctx.enter_context(tc.psum_pool(name="ps_s", bufs=1))
        ctx.enter_context(tc.manual_schedule())

        zeros = keep.tile([P, 512], BF16)
        nc.vector.memset(zeros[:].bitcast(I32), 0)

        def keep_busy(count):
            idle_bank = ps_x.tile([P, 512], F32, tag="x")
            for repeat in range(count):
                nc.tensor.matmul(out=idle_bank[:], lhsT=zeros[:, 0:P], rhs=zeros[:], start=True, stop=True)

        keep_busy(4)

        w1_rows = W1.rearrange("(p t) k -> p t k", t=4)
        w1_raw0 = keep.tile([P, 2, 512], BF16)
        w1_raw1 = keep.tile([P, 2, 512], BF16)
        w1_raw = [w1_raw0, w1_raw1]
        obj_rows = objs.rearrange("(h p) o d -> h p (o d)", p=P)
        obj_raw00 = keep.tile([P, 1024], BF16)
        obj_raw01 = keep.tile([P, 1024], BF16)
        obj_raw10 = keep.tile([P, 1024], BF16)
        obj_raw11 = keep.tile([P, 1024], BF16)
        obj_raw = [[obj_raw00, obj_raw01], [obj_raw10, obj_raw11]]
        b1_raw = keep.tile([P, 4], BF16)

        def load_w1(half):
            nc.sync.dma_start(out=w1_raw[half][:], in_=w1_rows[:, 2 * half : 2 * half + 2, :])

        def load_objects(half):
            for h in range(2):
                nc.sync.dma_start(out=obj_raw[half][h][:], in_=obj_rows[h, :, 1024 * half : 1024 * half + 1024])

        load_w1(0)
        load_objects(0)
        load_w1(1)
        nc.sync.dma_start(out=b1_raw[:], in_=b1.rearrange("(p t) -> p t", t=4))
        load_objects(1)
        w2_raw = keep.tile([P, 512], BF16)
        nc.sync.dma_start(out=w2_raw[:], in_=W2)
        b2_raw = keep.tile([P, P], BF16)
        nc.sync.dma_start(out=b2_raw[:], in_=b2.partition_broadcast(P))
        b2_col_raw = keep.tile([P, 1], BF16)
        nc.sync.dma_start(out=b2_col_raw[:], in_=b2.rearrange("(p o) -> p o", o=1))
        b2_col = keep.tile([P, 1], F32)

        ident = keep.tile([P, P], F32)
        make_identity(nc, ident[:])

        rot_codes = {}
        rot_scales = {}
        codes1 = keep.tile([P, OBJ * SETS], U32, align_bytes=64)
        scales1 = keep.tile([P, OBJ * SETS], U8, align_bytes=64)
        rot_codes[1] = codes1
        rot_scales[1] = scales1
        nc.vector.memset(scales1[:].bitcast(I32), 0)
        w1_codes0 = keep.tile([P, 4 * P], U32, align_bytes=64)
        w1_scales0 = keep.tile([P, 4 * P], U8, align_bytes=64)
        w1_codes1 = keep.tile([P, 4 * P], U32, align_bytes=64)
        w1_scales1 = keep.tile([P, 4 * P], U8, align_bytes=64)
        w1_codes = [w1_codes0, w1_codes1]
        w1_scales = [w1_scales0, w1_scales1]
        nc.vector.memset(w1_scales0[:].bitcast(I32), 0)

        w1_grp = keep.tile([P, 4 * P * 4], BF16, align_bytes=64)
        w1_grp_v = w1_grp[:].bitcast(F32).rearrange("p (t c u) -> p t c u", t=4, u=2)
        w1_words = [
            w1_raw[half][:].rearrange("p t k -> p (t k)").bitcast(F32).rearrange("p (t c u) -> p t c u", t=2, u=2)
            for half in range(2)
        ]
        obj_grp = keep.tile([P, 4 * SETS * 4], BF16, align_bytes=64)
        obj_grp_v = obj_grp[:].bitcast(F32).rearrange("p (s h c u) -> p s h c u", s=4, h=2, u=2)
        obj_words = [
            [obj_raw[half][h][:].bitcast(F32).rearrange("p (s c u) -> p s c u", s=2, u=2) for h in range(2)]
            for half in range(2)
        ]
        w2_grp = keep.tile([P, P * 4], BF16, align_bytes=64)
        w2_words = w2_raw[:].bitcast(F32).rearrange("p (c u) -> p c u", u=2)
        w2_codes = keep.tile([P, P], U32, align_bytes=64)
        w2_scales = keep.tile([P, P], U8, align_bytes=64)
        b1_f = keep.tile([P, 4], F32)
        b2_f = keep.tile([P, P], F32)

        def copy_out(engine, dst, src):
            if engine == "v":
                nc.vector.tensor_copy(out=dst, in_=src)
            else:
                nc.scalar.copy(out=dst, in_=src)

        def obj_quantise(s):
            nc.vector.quantize_mx(
                out=codes1[:, 512 * s : 512 * s + SETS].bitcast(FP8X4),
                scales=scales1[:, 512 * s : 512 * s + SETS],
                in_=obj_grp[:, 1024 * s : 1024 * s + 1024],
            )

        def w1_transposes(half):
            bank = ps_x.tile([P, 4, P], F32, tag="x")
            for t in range(2):
                for u in range(2):
                    nc.tensor.transpose(bank[:, 2 * t + u, :], w1_words[half][:, t, :, u], ident[:])
            return bank

        def w1_copy(half, engine, bank):
            copy_out(
                engine, w1_grp_v[:, 2 * half : 2 * half + 2], bank[:].rearrange("p (t u) c -> p t c u", u=2)
            )

        def w1_quantise(half):
            cols = slice(2 * P * half, 2 * P * half + 2 * P)
            nc.vector.quantize_mx(
                out=w1_codes0[:, cols].bitcast(FP8X4),
                scales=w1_scales0[:, cols],
                in_=w1_grp[:, 1024 * half : 1024 * half + 1024],
            )
            for dst_t, src_t in ((w1_codes1, w1_codes0), (w1_scales1, w1_scales0)):
                dv = dst_t[:, cols].bitcast(I32)
                sv = src_t[:, cols].bitcast(I32)
                nc.sync.dma_start(out=dv[0:64, :], in_=sv[64:128, :])
                nc.sync.dma_start(out=dv[64:128, :], in_=sv[0:64, :])

        def object_transposes(half, h, bank):
            for s in range(2):
                for u in range(2):
                    nc.tensor.transpose(bank[:, 2 * s + u, :], obj_words[half][h][:, s, :, u], ident[:])

        def object_copy(half, h, engine, bank):
            copy_out(
                engine, obj_grp_v[:, 2 * half : 2 * half + 2, h], bank[:].rearrange("p (s u) c -> p s c u", u=2)
            )

        w1_bank0 = w1_transposes(0)
        obj_bank00 = ps_x.tile([P, 4, P], F32, tag="x")
        object_transposes(0, 0, obj_bank00)
        obj_bank01 = ps_x.tile([P, 4, P], F32, tag="x")
        object_transposes(0, 1, obj_bank01)
        w1_bank1 = w1_transposes(1)
        obj_bank10 = ps_y.tile([P, 4, P], F32, tag="y")
        object_transposes(1, 0, obj_bank10)
        obj_bank11 = ps_y.tile([P, 4, P], F32, tag="y")
        object_transposes(1, 1, obj_bank11)
        w1_copy(0, "v", w1_bank0)
        object_copy(0, 0, "s", obj_bank00)
        w1_quantise(0)
        object_copy(0, 1, "v", obj_bank01)
        w1_copy(1, "s", w1_bank1)
        obj_quantise(0)
        obj_quantise(1)
        nc.vector.tensor_copy(out=b1_f[:], in_=b1_raw[:])
        w1_quantise(1)
        object_copy(1, 0, "s", obj_bank10)
        object_copy(1, 1, "v", obj_bank11)
        obj_quantise(2)
        obj_quantise(3)
        for t_ in (codes1, scales1):
            v4 = t_[:].bitcast(I32).rearrange("p (s e w) -> p s e w", s=4, e=2)
            nc.sync.dma_start(out=v4[0:64, :, 1, :], in_=v4[64:128, :, 0, :])
            nc.sync.dma_start(out=v4[64:128, 0:3, 1, :], in_=v4[0:64, 1:4, 0, :])
            nc.sync.dma_start(out=v4[64:128, 3, 1, :], in_=v4[0:64, 0, 0, :])
        def make_rotated(r):
            rc = rotp.tile([P, OBJ * SETS], U32, tag="rc", align_bytes=64)
            rs = rotp.tile([P, OBJ * SETS], U8, tag="rs", align_bytes=64)
            rot_codes[r] = rc
            rot_scales[r] = rs
            shift = (r - 1) % OBJ
            for dst_t, src_t, w in ((rc, codes1, SETS), (rs, scales1, SETS // 4)):
                dv = dst_t[:].bitcast(I32)
                sv = src_t[:].bitcast(I32)
                nc.sync.dma_start(out=dv[0:64, :], in_=sv[0:64, :])
                cut = (OBJ - shift) * w
                nc.sync.dma_start(out=dv[64:128, 0:cut], in_=sv[64:128, shift * w : OBJ * w])
                nc.sync.dma_start(out=dv[64:128, cut : OBJ * w], in_=sv[64:128, 0 : shift * w])

        out_rows = out_0.rearrange("(h p) q g -> p h q g", p=P)
        sum_t = ps_s.tile([P, 2, P], F32)

        chunks = []
        for blocks in (((0, 2), (4, 6)), ((1, 3), (5, 7))):
            for swap in (0, 1):
                for pair_of_blocks in blocks:
                    chunks.append((1, swap, pair_of_blocks))
        for r, swaps in ((2, (0, 1)), (3, (0, 1)), (4, (0,)), (0, (0,))):
            for swap in swaps:
                for jj in range(4):
                    chunks.append((r, swap, (2 * jj, 2 * jj + 1)))
        r_last, swap_last, blocks_last = chunks.pop()
        for block in blocks_last:
            chunks.append((r_last, swap_last, (block,)))
        n = len(chunks)
        st = {}

        def layer1(i):
            r, swap, blocks = chunks[i]
            width = SETS * len(blocks)
            hid = work.tile([P, 4, 512], BF16, tag="hid")
            if blocks[-1] == blocks[0] + len(blocks) - 1:
                parts = ((0, width, SETS * blocks[0]),)
            else:
                parts = tuple((SETS * q, SETS, SETS * blocks[q]) for q in range(2))
            for t in range(4):
                x = ps_x.tile([P, 512], F32, tag="x")
                for o0, part, c0 in parts:
                    nc.tensor.matmul_mx(
                        out=x[:, o0 : o0 + part],
                        lhsT=w1_codes[swap][:, P * t : P * t + P].bitcast(FP8X4),
                        lhsT_scale=w1_scales[swap][:, P * t : P * t + P],
                        rhs=rot_codes[r][:, c0 : c0 + part].bitcast(FP8X4),
                        rhs_scale=rot_scales[r][:, c0 : c0 + part],
                        start=True,
                        stop=True,
                    )
                if i == 0 and t == 3:
                    nc.vector.tensor_scalar(
                        out=hid[:, t, :width], in0=x[:, :width], scalar1=b1_f[:, t : t + 1], scalar2=0.0, op0=ALU.add, op1=ALU.max
                    )
                else:
                    nc.scalar.activation(out=hid[:, t, :width], in_=x[:, :width], func=ACT.Relu, bias=b1_f[:, t : t + 1], scale=1.0)
            st[("hid", i)] = hid

        def regroup(i, engine="v"):
            hid = st[("hid", i)]
            width = SETS * len(chunks[i][2])
            grp = work.tile([P, 512, 4], BF16, tag="grp", align_bytes=64)
            copy_out(
                engine,
                grp[:, :width, :].rearrange("p (c i) t -> p c t i", i=4),
                hid[:, :, :width].rearrange("p t (c i) -> p c t i", i=4),
            )
            st[("grp", i)] = grp

        def quantise(i):
            grp = st[("grp", i)]
            width = SETS * len(chunks[i][2])
            hc = work.tile([P, 512], U32, tag="hc", align_bytes=64)
            hs = work.tile([P, 512], U8, tag="hs", align_bytes=64)
            nc.vector.quantize_mx(
                out=hc[:, :width].bitcast(FP8X4),
                scales=hs[:, :width],
                in_=grp[:].rearrange("p w t -> p (w t)")[:, : 4 * width],
            )
            st[("h", i)] = (hc, hs)

        def layer2(i):
            hc, hs = st[("h", i)]
            count = len(chunks[i][2])
            y = ps_y.tile([P, 4, P], F32, tag="y")
            for h in range(2):
                for q in range(count):
                    c0 = SETS * q + P * h
                    nc.tensor.matmul_mx(
                        out=y[:, count * h + q, :],
                        lhsT=hc[:, c0 : c0 + P].bitcast(FP8X4),
                        lhsT_scale=hs[:, c0 : c0 + P],
                        rhs=w2_codes[:].bitcast(FP8X4),
                        rhs_scale=w2_scales[:],
                        start=True,
                        stop=True,
                    )
            st[("y", i)] = y

        def is_turned(i):
            return i % 5 == 2 and i < n - 5

        def layer2_turned(i):
            hc, hs = st[("h", i)]
            y = ps_y.tile([P, 4, P], F32, tag="y")
            nc.tensor.matmul_mx(
                out=y[:].rearrange("p j c -> p (j c)"),
                lhsT=w2_codes[:].bitcast(FP8X4),
                lhsT_scale=w2_scales[:],
                rhs=hc[:].bitcast(FP8X4),
                rhs_scale=hs[:],
                start=True,
                stop=True,
            )
            st[("y", i)] = y

        def relu_turned(i):
            turned = work.tile([P, 512], F32, tag="turned")
            nc.scalar.activation(
                out=turned[:], in_=st[("y", i)][:].rearrange("p j c -> p (j c)"), func=ACT.Relu, bias=b2_col[:], scale=1.0
            )
            st[("turned", i)] = turned

        def turn_back(i):
            turned = st[("turned", i)]
            z = ps_y.tile([P, 4, P], F32, tag="y")
            for h in range(2):
                for q in range(2):
                    c0 = SETS * q + P * h
                    nc.tensor.transpose(z[:, 2 * h + q, :], turned[:, c0 : c0 + P], ident[:])
            st[("z", i)] = z

        def bias2(i):
            y = st[("y", i)]
            slots = 2 * len(chunks[i][2])
            z = work.tile([P, 512], F32, tag="z")
            nc.vector.tensor_tensor(
                out=z[:, : slots * P].rearrange("p (j g) -> p j g", g=P),
                in0=y[:, :slots, :],
                in1=b2_f[:].unsqueeze(1).to_broadcast([P, slots, P]),
                op=ALU.add,
            )
            st[("z", i)] = z

        def finish(i):
            r, swap, blocks = chunks[i]
            z = st[("z", i)]
            count = len(blocks)
            width = SETS * count
            xo = outp.tile([P, 512], F32, tag="xo")
            if is_turned(i):
                nc.scalar.copy(out=xo[:], in_=z[:].rearrange("p j g -> p (j g)"))
            elif i < n - 5:
                nc.vector.tensor_scalar_max(out=xo[:, :width], in0=z[:, :width], scalar1=0.0)
            else:
                nc.scalar.activation(out=xo[:, :width], in_=z[:, :width], func=ACT.Relu)
            xo_v = xo[:, :width].rearrange("p (h q g) -> p h q g", h=2, q=count)
            for q in range(count):
                top = blocks[q]
                bot = (top + r) % OBJ
                m, k = (top, bot) if swap == 0 else (bot, top)
                nc.sync.dma_start(out=out_rows[:, :, OBJ * k + m, :], in_=xo_v[:, :, q, :])
            st[("xo", i)] = xo

        def add_up(i):
            xo = st[("xo", i)]
            for h in range(2):
                for q in range(2):
                    c0 = (2 * h + q) * P
                    nc.tensor.matmul(
                        out=sum_t[:, h, :],
                        lhsT=xo[:, c0 : c0 + P],
                        rhs=ident[:],
                        start=(i == 0 and h == 0 and q == 0),
                        stop=(i == n - 4 and h == 1 and q == 1),
                        is_transpose=True,
                    )

        def prepare_w2():
            p2 = ps_y.tile([P, 4, P], F32, tag="y")
            for u in range(2):
                nc.tensor.transpose(p2[:, u, :], w2_words[:, :, u], ident[:])
            copy_out("s", w2_grp[:].bitcast(F32).rearrange("p (c u) -> p c u", u=2), p2[:, 0:2, :].rearrange("p u c -> p c u"))

        def quantise_w2():
            nc.vector.quantize_mx(out=w2_codes[:].bitcast(FP8X4), scales=w2_scales[:], in_=w2_grp[:])
            nc.vector.tensor_copy(out=b2_f[:], in_=b2_raw[:])
            nc.vector.tensor_copy(out=b2_col[:], in_=b2_col_raw[:])

        sum_sb = keep.tile([P, 2, P], F32)

        def turn_sums_back():
            back = ps_x.tile([P, 4, P], F32, tag="x")
            for h in range(2):
                nc.tensor.transpose(back[:, h, :], sum_sb[:, h, :], ident[:])
            st["back"] = back

        def add_to_sums(part, i=None, so_far=None):
            sums = work.tile([P, 2, P], F32, tag="sums")
            if i is None:
                nc.vector.tensor_tensor(out=sums[:], in0=part, in1=so_far, op=ALU.add)
            else:
                z_v = st[("z", i)][:, :SETS].rearrange("p (h g) -> p h g", g=P)
                nc.vector.scalar_tensor_tensor(out=sums[:], in0=z_v, scalar=0.0, in1=part, op0=ALU.max, op1=ALU.add)
            return sums

        rotate_at = {0: 2, 6: 3, 12: 4, 17: 0}
        for i in range(n):
            if i in rotate_at:
                make_rotated(rotate_at[i])
            layer1(i)
            if i == n - 1:
                regroup(i, "s")
            if i == 1:
                prepare_w2()
            if i == 2:
                quantise_w2()
            if i >= 3 and is_turned(i - 3):
                layer2_turned(i - 3)
                relu_turned(i - 3)
            elif i >= 3:
                layer2(i - 3)
            if i >= 4 and is_turned(i - 4):
                turn_back(i - 4)
            if i >= 5:
                add_up(i - 5)
            if i >= 1:
                regroup(i - 1)
            if i >= 3 and not is_turned(i - 3):
                bias2(i - 3)
            if i >= 3 and is_turned(i - 3):
                finish(i - 4)
                quantise(i - 1)
            else:
                if i >= 1:
                    quantise(i - 1)
                if i >= 4:
                    finish(i - 4)

        layer2(n - 3)
        keep_busy(3)
        bias2(n - 3)
        quantise(n - 1)
        finish(n - 4)
        layer2(n - 2)
        layer2(n - 1)
        add_up(n - 5)
        add_up(n - 4)
        bias2(n - 2)
        finish(n - 3)
        bias2(n - 1)
        nc.scalar.copy(out=sum_sb[:], in_=sum_t[:])
        finish(n - 2)
        finish(n - 1)
        xo_v = st[("xo", n - 3)][:].rearrange("p (h q g) -> p h q g", h=2, q=2)
        first = add_to_sums(xo_v[:, :, 0, :], i=n - 2)
        second = add_to_sums(xo_v[:, :, 1, :], i=n - 1)
        turn_sums_back()
        both = add_to_sums(first[:], so_far=second[:])
        total = add_to_sums(st["back"][:, 0:2, :], so_far=both[:])
        nc.sync.dma_start(out=out_1.rearrange("(h p) g -> p h g", p=P), in_=total[:])
